import numpy as np
import ml_dtypes


def mxq(x, axis, fmt="e4m3"):
    dtype, down = {"e4m3": (ml_dtypes.float8_e4m3fn, 7), "e5m2": (ml_dtypes.float8_e5m2, 14)}[fmt]
    v = np.moveaxis(np.asarray(x, np.float32).astype(ml_dtypes.bfloat16).astype(np.float64), axis, -1)
    blocks = v.reshape(v.shape[:-1] + (-1, 32))
    amax = np.abs(blocks).max(-1, keepdims=True)
    byte = np.maximum(np.where(amax > 0, np.frexp(amax)[1] - 1 + 127, 0) - down, 1)
    scale = np.exp2(byte - 127.0)
    codes = (blocks / scale).astype(np.float32).astype(dtype).astype(np.float64)
    return np.moveaxis((codes * scale).reshape(v.shape), -1, axis)


WIDE = False


def mx_kscale(k):
    if not WIDE:
        return np.ones(k)
    levels = np.array([10, -10, 5, -5, 0])
    if k % 512:
        return np.exp2(np.random.permutation(np.resize(levels, k // 32))).repeat(32)
    a = np.empty((k // 512, 16))
    for p in range(k // 512):
        a[p, :8] = np.random.permutation(np.resize(levels, 8))
        for g in range(8):
            far = levels[np.abs(levels - a[p, g]) >= 10]
            a[p, g + 8] = far[np.random.randint(len(far))]
    return np.exp2(a.ravel()).repeat(32)


BF16 = ml_dtypes.bfloat16


def bf(x):
    return np.asarray(x, np.float32).astype(BF16)


def f64(x):
    return np.asarray(x).astype(np.float64)


B, D, C = 1536, 1024, 1024
SCALE = 100.0
GAMMA = 20.0
EPS = 1e-12
PULL = 2.0
KSCALE = 4.0
GSCALE = 8192.0


def l2_normalize(v, axis):
    sq = np.sum(v * v, axis=axis, keepdims=True)
    return v * (1.0 / np.sqrt(np.maximum(sq, EPS)))


def rbf_and_probs(x, kernel):
    e = l2_normalize(x, 1)
    w = l2_normalize(kernel, 0)
    dots = e @ w
    r = np.exp(-(2.0 - 2.0 * dots) / GAMMA)
    logits = SCALE * r
    z = np.exp(logits - logits.max(-1, keepdims=True))
    return r, z / z.sum(-1, keepdims=True)


def setup_inputs():
    s = mx_kscale(B)[:, None]
    u = mx_kscale(C)[None, :]
    gm = np.random.standard_normal((D, C))
    lab = np.random.randint(0, C, B)
    x0 = bf(PULL * gm[:, lab].T + np.random.standard_normal((B, D)))
    kernel0 = bf(gm * (KSCALE / np.sqrt(D)))
    g = bf(np.random.standard_normal((B, C)) * np.exp2(np.random.randint(-6, 1, (B, 1))) * GSCALE)
    r, p = rbf_and_probs(f64(x0), f64(kernel0))
    return {"x": bf(f64(x0) * s), "kernel": bf(f64(kernel0) / u), "rbf": np.asarray(r, np.float32),
            "probs": np.asarray(p, np.float32), "grad_out": g}


def reference(x, kernel, rbf, probs, grad_out):
    xf = f64(x)
    kf = f64(kernel)
    p = f64(probs)
    g = f64(grad_out)
    rx = 1.0 / np.sqrt(np.maximum(np.sum(xf * xf, axis=1, keepdims=True), EPS))
    rk = 1.0 / np.sqrt(np.maximum(np.sum(kf * kf, axis=0, keepdims=True), EPS))
    e = xf * rx
    w = kf * rk
    dl = p * (g - np.sum(g * p, axis=1, keepdims=True))
    dz = dl * (SCALE * 2.0 / GAMMA) * f64(rbf) * rx * rk
    a = mxq(dz, 1, "e5m2") @ mxq(kf, 1, "e4m3").T
    c = mxq(xf, 0, "e4m3").T @ mxq(dz, 0, "e5m2")
    dx = a - e * np.sum(a * e, axis=1, keepdims=True)
    dk = c - w * np.sum(c * w, axis=0, keepdims=True)
    return dx, dk

@@ -1,0 +1,435 @@
+from contextlib import ExitStack
+
+import concourse.mybir as mybir
+from concourse.masks import make_identity
+
+B, D, C = 1536, 1024, 1024
+FLOPS = 2 * 2 * B * D * C
+
+F32 = mybir.dt.float32
+BF16 = mybir.dt.bfloat16
+U32 = mybir.dt.uint32
+U8 = mybir.dt.uint8
+E4 = mybir.dt.float8_e4m3fn_x4
+E5 = mybir.dt.float8_e5m2_x4
+ALU = mybir.AluOpType
+ACT = mybir.ActivationFunctionType
+
+P = 128
+NG = 3
+J = 4
+NT = NG * J
+NPAIR = NT // 2
+H = 512
+EPS = 1e-12
+NGRAM = 5
+
+MANUAL = False
+
+
+def tile_rbf_softmax_layer_t_v_kernel(tc, x, kernel, rbf, probs, grad_out, out_0, out_1):
+    nc = tc.nc
+    x_v = x.rearrange("(g p j) w -> p g j w", p=P, j=J)
+    go_v = grad_out.rearrange("(g p j) w -> p g j w", p=P, j=J)
+    pr_v = probs.rearrange("(g p j) w -> p g j w", p=P, j=J)
+    rb_v = rbf.rearrange("(g p j) w -> p g j w", p=P, j=J)
+    o0_v = out_0.rearrange("(g p j) w -> p g j w", p=P, j=J)
+    k_v = kernel.rearrange("(a p) c -> p a c", p=P)
+    o1_v = out_1.rearrange("(a p) c -> p a c", p=P)
+
+    with ExitStack() as ctx:
+        keep = ctx.enter_context(tc.tile_pool(name="keep", bufs=1))
+        st = ctx.enter_context(tc.tile_pool(name="st", bufs=6))
+        ilv = ctx.enter_context(tc.tile_pool(name="ilv", bufs=3))
+        gpool = ctx.enter_context(tc.tile_pool(name="gpool", bufs=2))
+        ppool = ctx.enter_context(tc.tile_pool(name="ppool", bufs=6))
+        rpool = ctx.enter_context(tc.tile_pool(name="rpool", bufs=6))
+        dzpool = ctx.enter_context(tc.tile_pool(name="dzpool", bufs=2))
+        tgpool = ctx.enter_context(tc.tile_pool(name="tgpool", bufs=2))
+        tcpool = ctx.enter_context(tc.tile_pool(name="tcpool", bufs=2))
+        psum = ctx.enter_context(tc.psum_pool(name="psum", bufs=1))
+        if MANUAL:
+            ctx.enter_context(tc.manual_schedule())
+
+        def bank(b, shape, dtype, nm):
+            return psum.tile(shape, dtype, name="%s_b%d" % (nm, b), tag="b%d" % b)
+
+        one = keep.tile([P, 1], F32, name="one")
+        nc.vector.memset(one[:], 1.0)
+        warm = keep.tile([P, 1], F32, name="warm")
+        nc.scalar.activation(out=warm[:], in_=one[:], func=ACT.Sqrt)
+        ident_b = keep.tile([P, P], BF16, name="ident_b")
+        make_identity(nc, ident_b[:])
+        ident_f = keep.tile([P, P], F32, name="ident_f")
+        make_identity(nc, ident_f[:])
+
+        junk_v = keep.tile([P, C], F32, name="junk_v")
+        junk_s = keep.tile([P, C], BF16, name="junk_s")
+
+        ktn = keep.tile([P, 8, D], BF16, name="ktn")
+        ktc = keep.tile([P, 2, D], U32, name="ktc", align_bytes=64)
+        kts = keep.tile([P, 2, D], U8, name="kts", align_bytes=64)
+        xc = keep.tile([P, NG, D], U32, name="xc", align_bytes=64)
+        xs = keep.tile([P, NG, D], U8, name="xs", align_bytes=64)
+        dzc = keep.tile([P, NG, C], U32, name="dzc", align_bytes=64)
+        dzs = keep.tile([P, NG, C], U8, name="dzs", align_bytes=64)
+        rkb = keep.tile([P, C], F32, name="rkb")
+
+        ssk = keep.tile([P, 16], F32, name="ssk")
+        tk = keep.tile([P, 16], F32, name="tk")
+        nrk2 = keep.tile([P, 16], F32, name="nrk2")
+        rk10 = keep.tile([P, 16], F32, name="rk10")
+        ssx = keep.tile([P, NT], F32, name="ssx")
+        tx = keep.tile([P, NT], F32, name="tx")
+        nrx2 = keep.tile([P, NT], F32, name="nrx2")
+        rx = keep.tile([P, NT], F32, name="rx")
+        s_all = keep.tile([P, NT], F32, name="s_all")
+        sg2 = keep.tile([P, 2 * NT], F32, name="sg2")
+        sg = keep.tile([P, NT], F32, name="sg")
+        cg2 = keep.tile([P, 16], F32, name="cg2")
+        cg = keep.tile([P, 8], F32, name="cg")
+
+        nc.vector.memset(ssk[:], 1.0)
+
+        def cm(m):
+            return m if m < 6 else m + 2
+
+        xr = [keep.tile([P, J, D], BF16, name="xr%d" % g) for g in range(NG)]
+        gr = [None] * NG
+        pt = [None] * NT
+        rb = [None] * NT
+
+        def load_x(g, j0, j1):
+            nc.sync.dma_start(out=xr[g][:, j0:j1, :], in_=x_v[:, g, j0:j1, :])
+
+        def alloc_g(g):
+            gr[g] = gpool.tile([P, J, C], BF16, name="gr", tag="gr")
+
+        def load_g(g, j0, j1):
+            nc.sync.dma_start(out=gr[g][:, j0:j1, :], in_=go_v[:, g, j0:j1, :])
+
+        def load_p(r):
+            pt[r] = ppool.tile([P, C], F32, name="pt", tag="pt")
+            nc.sync.dma_start(out=pt[r][:], in_=pr_v[:, r // J, r % J, :])
+
+        def load_r(r):
+            rb[r] = rpool.tile([P, C], F32, name="rb", tag="rb")
+            nc.sync.dma_start(out=rb[r][:], in_=rb_v[:, r // J, r % J, :])
+
+        load_x(0, 0, 2)
+        kraw = []
+        for c in range(4):
+            t = st.tile([P, 2, C], BF16, name="kraw%d" % c, tag="st")
+            nc.sync.dma_start(out=t[:], in_=k_v[:, 2 * c : 2 * c + 2, :])
+            kraw.append(t)
+        alloc_g(0)
+        alloc_g(1)
+        load_r(0)
+        load_p(0)
+        load_g(0, 0, 2)
+        load_r(1)
+        load_p(1)
+        load_x(0, 2, 4)
+        load_r(2)
+        load_p(2)
+        load_g(0, 2, 4)
+        load_r(3)
+        load_p(3)
+        load_x(1, 0, 4)
+        load_r(4)
+        load_p(4)
+        load_g(1, 0, 4)
+        load_r(5)
+        load_p(5)
+        load_x(2, 0, 4)
+
+        def rx_sq(r):
+            nc.scalar.activation(out=junk_s[:], in_=xr[r // J][:, r % J, :], func=ACT.Square, accum_out=ssx[:, r : r + 1])
+
+        def rx_fin(c0, c1):
+            nc.vector.tensor_scalar(out=tx[:, c0:c1], in0=ssx[:, c0:c1], scalar1=EPS, scalar2=-1.0, op0=ALU.max, op1=ALU.mult)
+            nc.vector.reciprocal(out=nrx2[:, c0:c1], in_=tx[:, c0:c1])
+            nc.scalar.activation(out=rx[:, c0:c1], in_=nrx2[:, c0:c1], func=ACT.Sqrt, scale=-1.0)
+
+        rx_sq(0)
+        rx_sq(1)
+        rx_fin(0, 2)
+
+        gb = [bank(m, [P, P], F32, "gb") for m in range(NGRAM)]
+        kb = [None] * 8
+        for m in range(NGRAM, 8):
+            kb[m] = bank(m, [P, D], BF16, "kb")
+        for a in range(8):
+            ka = kraw[a // 2][:, a % 2, :]
+            for m in range(NGRAM):
+                nc.tensor.matmul(out=gb[m][:], lhsT=ka[:, m * P : (m + 1) * P], rhs=ka[:, m * P : (m + 1) * P], start=(a == 0), stop=(a == 7))
+            for m in range(NGRAM, 8):
+                nc.tensor.transpose(kb[m][:, a * P : (a + 1) * P], ka[:, m * P : (m + 1) * P], ident_b[:])
+        for m in range(NGRAM):
+            nc.vector.scalar_tensor_tensor(out=junk_v[:, 0:P], in0=gb[m][:], scalar=1.0, in1=ident_f[:], op0=ALU.mult, op1=ALU.mult, accum_out=ssk[:, m : m + 1])
+        nc.vector.tensor_copy(out=ktn[:, 5, :], in_=kb[5][:])
+        nc.vector.scalar_tensor_tensor(out=junk_v[:], in0=kb[5][:], scalar=1.0, in1=ktn[:, 5, :], op0=ALU.mult, op1=ALU.mult, accum_out=ssk[:, 5:6])
+        for m in (6, 7):
+            nc.scalar.activation(out=junk_s[:], in_=kb[m][:], func=ACT.Square, accum_out=ssk[:, cm(m) : cm(m) + 1])
+        nc.vector.scalar_tensor_tensor(out=rb[0][:], in0=pt[0][:], scalar=rx[:, 0:1], in1=rb[0][:], op0=ALU.mult, op1=ALU.mult)
+        nc.vector.tensor_scalar(out=tk[:], in0=ssk[:], scalar1=EPS, scalar2=-1.0, op0=ALU.max, op1=ALU.mult)
+        nc.vector.reciprocal(out=nrk2[:], in_=tk[:])
+        nc.scalar.activation(out=rk10[:], in_=nrk2[:], func=ACT.Sqrt, scale=-100.0)
+        rp = [bank(2, [P, H], F32, "rp"), bank(3, [P, H], F32, "rp")]
+        for m in range(8):
+            nc.tensor.matmul(out=rp[m // 4][:, (m % 4) * P : (m % 4 + 1) * P], lhsT=rk10[:, cm(m) : cm(m) + 1].to_broadcast([P, P]), rhs=ident_f[:], start=True, stop=True)
+        nc.scalar.copy(out=rkb[:, 0:H], in_=rp[0][:])
+        nc.vector.tensor_copy(out=rkb[:, H:C], in_=rp[1][:])
+        nc.vector.tensor_tensor(out=rb[0][:], in0=rb[0][:], in1=rkb[:], op=ALU.mult)
+
+        def s_scale(r):
+            nc.scalar.activation(out=rb[r][:], in_=rb[r][:], func=ACT.Copy, scale=rx[:, r : r + 1])
+
+        def g_mul(r):
+            nc.gpsimd.tensor_tensor(out=rb[r][:], in0=pt[r][:], in1=rb[r][:], op=ALU.mult)
+            nc.gpsimd.tensor_tensor(out=rb[r][:], in0=rb[r][:], in1=rkb[:], op=ALU.mult)
+
+        s_scale(1)
+        g_mul(1)
+        for m in (6, 7):
+            nc.scalar.copy(out=ktn[:, m, :], in_=kb[m][:])
+
+        gps = [None] * NT
+        dz = [None] * NG
+        dzg = [None] * NG
+        xg = [None] * NG
+        tgp = [None] * NPAIR
+        tcd = [None] * NPAIR
+        tsc = [None] * NPAIR
+        aps = [None] * NT
+        dx = [None] * NT
+
+        def gcopy(r):
+            gps[r] = bank(r % 2, [P, C], BF16, "gps")
+            for n in range(2):
+                nc.tensor.matmul(out=gps[r][:, H * n : H * n + H], lhsT=ident_b[:], rhs=gr[r // J][:, r % J, H * n : H * n + H], start=True, stop=True)
+
+        def op_a(r):
+            nc.vector.scalar_tensor_tensor(out=junk_v[:], in0=gps[r][:], scalar=1.0, in1=pt[r][:], op0=ALU.mult, op1=ALU.mult, accum_out=s_all[:, r : r + 1])
+
+        def op_f(r):
+            g = r // J
+            if r % J == 0:
+                dz[g] = dzpool.tile([P, J, C], BF16, name="dz", tag="dz")
+            nc.vector.scalar_tensor_tensor(out=dz[g][:, r % J, :], in0=gps[r][:], scalar=s_all[:, r : r + 1], in1=rb[r][:], op0=ALU.subtract, op1=ALU.mult)
+
+        def op_t(r):
+            d = r // 2
+            if r % 2 == 0:
+                tgp[d] = tgpool.tile([P, 2, 2, P, 4], BF16, name="tgp", tag="tgp", align_bytes=64)
+            tps = bank(2 + r % 2, [P, 2, 2, P], F32, "tps")
+            w = dz[r // J][:, r % J, :].bitcast(F32)
+            for h in range(2):
+                for u in range(2):
+                    nc.tensor.transpose(tps[:, h, u, :], w[:, 256 * h + u : 256 * (h + 1) : 2], ident_f[:])
+            dst = tgp[d][:, r % 2].rearrange("q h p t -> q (h p t)").bitcast(F32).rearrange("q (h p u) -> q h p u", h=2, u=2)
+            nc.scalar.copy(out=dst, in_=tps[:].rearrange("q h u p -> q h p u"))
+
+        def op_q(d):
+            tcd[d] = tcpool.tile([P, 4 * P], U32, name="tcd", tag="tcd", align_bytes=64)
+            tsc[d] = tcpool.tile([P, 4 * P], U8, name="tsc", tag="tsc", align_bytes=64)
+            nc.vector.quantize_mx(out=tcd[d][:].bitcast(E5), scales=tsc[d][:], in_=tgp[d][:].rearrange("q i h p t -> q (i h p t)"))
+
+        def op_mm(r):
+            d = r // 2
+            b0 = 4 + 2 * (r % 2)
+            aps[r] = [bank(b0, [P, H], F32, "aps"), bank(b0 + 1, [P, H], F32, "aps")]
+            for n in range(2):
+                for h in range(2):
+                    c0 = P * (2 * (r % 2) + h)
+                    nc.tensor.matmul_mx(
+                        out=aps[r][n][:],
+                        lhsT=tcd[d][:, c0 : c0 + P].bitcast(E5),
+                        lhsT_scale=tsc[d][:, c0 : c0 + P],
+                        rhs=ktc[:, h, H * n : H * n + H].bitcast(E4),
+                        rhs_scale=kts[:, h, H * n : H * n + H],
+                        start=(h == 0),
+                        stop=(h == 1),
+                    )
+
+        def op_e0a(r):
+            for n in range(2):
+                nc.vector.scalar_tensor_tensor(out=junk_v[:, 0:H], in0=aps[r][n][:], scalar=nrx2[:, r : r + 1], in1=xr[r // J][:, r % J, H * n : H * n + H], op0=ALU.mult, op1=ALU.mult, accum_out=sg2[:, 2 * r + n : 2 * r + n + 1])
+            nc.scalar.activation(out=sg[:, r : r + 1], in_=sg2[:, 2 * r : 2 * r + 1], func=ACT.Identity, bias=sg2[:, 2 * r + 1 : 2 * r + 2])
+
+        def op_e0b(r):
+            dx[r] = st.tile([P, D], F32, name="dx", tag="st")
+            for n in range(2):
+                nc.vector.scalar_tensor_tensor(out=dx[r][:, H * n : H * n + H], in0=xr[r // J][:, r % J, H * n : H * n + H], scalar=sg[:, r : r + 1], in1=aps[r][n][:], op0=ALU.mult, op1=ALU.add)
+            nc.sync.dma_start(out=o0_v[:, r // J, r % J, :], in_=dx[r][:])
+
+        def dzil(g):
+            dzg[g] = ilv.tile([P, C, J], BF16, name="dzg", tag="ilv", align_bytes=64)
+            for q in range(4):
+                ws = slice(256 * q, 256 * q + 256)
+                nc.scalar.copy(out=dzg[g][:, ws, :], in_=dz[g][:, :, ws].rearrange("p j w -> p w j"))
+
+        def qd(g):
+            nc.vector.quantize_mx(out=dzc[:, g, :].bitcast(E5), scales=dzs[:, g, :], in_=dzg[g][:].rearrange("p w j -> p (w j)"))
+
+        def xil(g):
+            xg[g] = ilv.tile([P, D, J], BF16, name="xg", tag="ilv", align_bytes=64)
+            for q in range(4):
+                ws = slice(256 * q, 256 * q + 256)
+                nc.gpsimd.tensor_scalar(out=xg[g][:, ws, :], in0=xr[g][:, :, ws].rearrange("p j w -> p w j"), scalar1=1.0, scalar2=0.0, op0=ALU.mult, op1=ALU.add)
+
+        def qx(g):
+            nc.vector.quantize_mx(out=xc[:, g, :].bitcast(E4), scales=xs[:, g, :], in_=xg[g][:].rearrange("p w j -> p (w j)"))
+
+        ring = [4, 5, 6, 7]
+        ring_at = [0]
+
+        def next_bank():
+            b = ring[ring_at[0] % 4]
+            ring_at[0] = ring_at[0] + 1
+            return b
+
+        def ktg_half(h):
+            ktg = ilv.tile([P, D, 4], BF16, name="ktg", tag="ilv", align_bytes=64)
+            ktw = ktg[:].rearrange("q f t -> q (f t)").bitcast(F32)
+            for c in range(4):
+                tb = bank(next_bank(), [P, 2, 2, P], F32, "tb")
+                for a2 in range(2):
+                    kw = kraw[c][:, a2, :].bitcast(F32)
+                    for u in range(2):
+                        nc.tensor.transpose(tb[:, a2, u, :], kw[:, 256 * h + u : 256 * (h + 1) : 2], ident_f[:])
+                dst = ktw[:, 512 * c : 512 * c + 512].rearrange("q (a f u) -> q a f u", a=2, u=2)
+                nc.vector.tensor_copy(out=dst, in_=tb[:].rearrange("q a u f -> q a f u"))
+            nc.vector.quantize_mx(out=ktc[:, h, :].bitcast(E4), scales=kts[:, h, :], in_=ktg[:].rearrange("q f t -> q (f t)"))
+
+        def ktn_block(m):
+            kbm = bank(next_bank(), [P, D], BF16, "kb")
+            for a in range(8):
+                nc.tensor.transpose(kbm[:, a * P : (a + 1) * P], kraw[a // 2][:, a % 2, m * P : (m + 1) * P], ident_b[:])
+            nc.vector.tensor_copy(out=ktn[:, m, :], in_=kbm[:])
+
+        gcopy(0)
+        gcopy(1)
+        rx_sq(2)
+        rx_sq(3)
+        rx_fin(2, 4)
+        s_scale(2)
+        g_mul(2)
+        s_scale(3)
+        g_mul(3)
+
+        cbanks = [(0, 1), (2, 3), (4, 5)]
+        cps = [None] * 8
+        dk = [None] * 8
+
+        def c_alloc(m):
+            b = cbanks[m % 3]
+            cps[m] = [bank(b[0], [P, H], F32, "cps"), bank(b[1], [P, H], F32, "cps")]
+
+        def c_mm(m, gs):
+            for n in range(2):
+                for g in gs:
+                    nc.tensor.matmul_mx(
+                        out=cps[m][n][:],
+                        lhsT=dzc[:, g, P * m : P * m + P].bitcast(E5),
+                        lhsT_scale=dzs[:, g, P * m : P * m + P],
+                        rhs=xc[:, g, H * n : H * n + H].bitcast(E4),
+                        rhs_scale=xs[:, g, H * n : H * n + H],
+                        start=(g == 0),
+                        stop=(g == NG - 1),
+                    )
+
+        for d in range(NPAIR + 2):
+            e = d - 2
+            if e >= 0:
+                op_e0a(2 * e)
+                op_e0a(2 * e + 1)
+                op_e0b(2 * e)
+                op_e0b(2 * e + 1)
+            if d == 0:
+                ktg_half(0)
+                ktg_half(1)
+            if d == 1:
+                for m in range(NGRAM):
+                    ktn_block(m)
+            if 1 <= d <= NPAIR:
+                op_q(d - 1)
+                op_mm(2 * d - 2)
+                op_mm(2 * d - 1)
+            if d == 7:
+                qd(2)
+                qx(2)
+            if d == 0:
+                for r in range(4, 8):
+                    rx_sq(r)
+                rx_fin(4, 8)
+            if d == 2:
+                for r in range(8, 12):
+                    rx_sq(r)
+                rx_fin(8, 12)
+            for r in (2 * d + 4, 2 * d + 5):
+                if r < NT:
+                    s_scale(r)
+                    g_mul(r)
+            if d == 6:
+                qx(0)
+                qx(1)
+            if d in (2, 4, 6):
+                dzil(d // 2 - 1)
+            if d in (4, 5, 6):
+                xil(d - 4)
+            if d == 6:
+                c_alloc(0)
+                c_mm(0, (0, 1))
+                c_alloc(1)
+                c_mm(1, (0, 1))
+            if d < NPAIR:
+                op_a(2 * d)
+                op_a(2 * d + 1)
+                for r in (2 * d, 2 * d + 1):
+                    if r + 6 < NT:
+                        load_p(r + 6)
+                for r in (2 * d, 2 * d + 1):
+                    op_f(r)
+                    if r + 6 < NT:
+                        load_r(r + 6)
+                    op_t(r)
+                if d + 1 < NPAIR:
+                    if d == 1:
+                        alloc_g(2)
+                        load_g(2, 0, 4)
+                    gcopy(2 * d + 2)
+                    gcopy(2 * d + 3)
+            if d in (3, 5):
+                qd(d // 2 - 1)
+
+        def e1a(m):
+            for n in range(2):
+                nc.vector.scalar_tensor_tensor(out=junk_v[:, 0:H], in0=cps[m][n][:], scalar=nrk2[:, cm(m) : cm(m) + 1], in1=ktn[:, m, H * n : H * n + H], op0=ALU.mult, op1=ALU.mult, accum_out=cg2[:, 2 * m + n : 2 * m + n + 1])
+            nc.scalar.activation(out=cg[:, m : m + 1], in_=cg2[:, 2 * m : 2 * m + 1], func=ACT.Identity, bias=cg2[:, 2 * m + 1 : 2 * m + 2])
+
+        def e1b(m):
+            dk[m] = st.tile([P, D], F32, name="dk", tag="st")
+            for n in range(2):
+                nc.vector.scalar_tensor_tensor(out=dk[m][:, H * n : H * n + H], in0=ktn[:, m, H * n : H * n + H], scalar=cg[:, m : m + 1], in1=cps[m][n][:], op0=ALU.mult, op1=ALU.add)
+            o1s = st.tile([P, 8, P], F32, name="o1s", tag="st")
+            for hf in range(2):
+                bt = bank(6 + hf, [P, 4, P], F32, "bt")
+                for a in range(4):
+                    nc.tensor.transpose(bt[:, a, :], dk[m][:, P * (4 * hf + a) : P * (4 * hf + a) + P], ident_f[:])
+                if m == 7 and hf == 1:
+                    nc.vector.tensor_copy(out=o1s[:, 4 * hf : 4 * hf + 4, :], in_=bt[:])
+                else:
+                    nc.scalar.copy(out=o1s[:, 4 * hf : 4 * hf + 4, :], in_=bt[:])
+            nc.sync.dma_start(out=o1_v[:, :, P * m : P * m + P], in_=o1s[:])
+
+        c_mm(0, (2,))
+        c_mm(1, (2,))
+        e1a(0)
+        for m in range(8):
+            if m + 2 < 8:
+                c_alloc(m + 2)
+                c_mm(m + 2, (0, 1, 2))
+            if m + 1 < 8:
+                e1a(m + 1)
+            e1b(m)

@@ -22,9 +22,20 @@ NT = NG * J
 NPAIR = NT // 2
 H = 512
 EPS = 1e-12
-NGRAM = 5
+NGRAM = 6
 
-MANUAL = False
+MANUAL = True
+KTG_ENG = "S"
+KTN_ENG = "S"
+XIL_S = False
+GSPLIT = 1
+GLEAD = 2
+RENDEZVOUS = True
+V_MUL = (0, 1)
+GP_E0 = ()
+GPC = False
+C_G = (0,)
+C_V = (1, 2, 3, 4, 5, 6, 7)
 
 
 def tile_rbf_softmax_layer_t_v_kernel(tc, x, kernel, rbf, probs, grad_out, out_0, out_1):
@@ -78,6 +89,9 @@ def tile_rbf_softmax_layer_t_v_kernel(tc, x, kernel, rbf, probs, grad_out, out_0
         ssk = keep.tile([P, 16], F32, name="ssk")
         tk = keep.tile([P, 16], F32, name="tk")
         nrk2 = keep.tile([P, 16], F32, name="nrk2")
+        rk2 = keep.tile([P, 16], F32, name="rk2")
+        rx2 = keep.tile([P, NT], F32, name="rx2")
+        tjunk = keep.tile([P, 8], F32, name="tjunk")
         rk10 = keep.tile([P, 16], F32, name="rk10")
         ssx = keep.tile([P, NT], F32, name="ssx")
         tx = keep.tile([P, NT], F32, name="tx")
@@ -116,89 +130,68 @@ def tile_rbf_softmax_layer_t_v_kernel(tc, x, kernel, rbf, probs, grad_out, out_0
             rb[r] = rpool.tile([P, C], F32, name="rb", tag="rb")
             nc.sync.dma_start(out=rb[r][:], in_=rb_v[:, r // J, r % J, :])
 
-        load_x(0, 0, 2)
-        kraw = []
-        for c in range(4):
-            t = st.tile([P, 2, C], BF16, name="kraw%d" % c, tag="st")
-            nc.sync.dma_start(out=t[:], in_=k_v[:, 2 * c : 2 * c + 2, :])
-            kraw.append(t)
+        dma_plan = [
+            ("k", 0), ("k", 1), ("k", 2), ("k", 3), ("x", 0, 0, 2), ("r", 0), ("p", 0), ("g", 0, 0, 2), ("r", 1), ("p", 1),
+            ("r", 2), ("p", 2), ("x", 0, 2, 4), ("g", 0, 2, 4), ("r", 3), ("p", 3), ("x", 1, 0, 4), ("r", 4), ("p", 4),
+            ("g", 1, 0, 4), ("r", 5), ("p", 5), ("x", 2, 0, 4),
+        ]
+        kraw = [None] * 4
         alloc_g(0)
         alloc_g(1)
-        load_r(0)
-        load_p(0)
-        load_g(0, 0, 2)
-        load_r(1)
-        load_p(1)
-        load_x(0, 2, 4)
-        load_r(2)
-        load_p(2)
-        load_g(0, 2, 4)
-        load_r(3)
-        load_p(3)
-        load_x(1, 0, 4)
-        load_r(4)
-        load_p(4)
-        load_g(1, 0, 4)
-        load_r(5)
-        load_p(5)
-        load_x(2, 0, 4)
+        for item in dma_plan:
+            if item[0] == "x":
+                load_x(item[1], item[2], item[3])
+            if item[0] == "g":
+                load_g(item[1], item[2], item[3])
+            if item[0] == "r":
+                load_r(item[1])
+            if item[0] == "p":
+                load_p(item[1])
+            if item[0] == "k":
+                c = item[1]
+                kraw[c] = st.tile([P, 2, C], BF16, name="kraw%d" % c, tag="st")
+                nc.sync.dma_start(out=kraw[c][:], in_=k_v[:, 2 * c : 2 * c + 2, :])
 
         def rx_sq(r):
             nc.scalar.activation(out=junk_s[:], in_=xr[r // J][:, r % J, :], func=ACT.Square, accum_out=ssx[:, r : r + 1])
 
-        def rx_fin(c0, c1):
-            nc.vector.tensor_scalar(out=tx[:, c0:c1], in0=ssx[:, c0:c1], scalar1=EPS, scalar2=-1.0, op0=ALU.max, op1=ALU.mult)
-            nc.vector.reciprocal(out=nrx2[:, c0:c1], in_=tx[:, c0:c1])
-            nc.scalar.activation(out=rx[:, c0:c1], in_=nrx2[:, c0:c1], func=ACT.Sqrt, scale=-1.0)
+        def rx_fin_v(c0, c1):
+            nc.vector.tensor_scalar(out=tx[:, c0:c1], in0=ssx[:, c0:c1], scalar1=EPS, scalar2=None, op0=ALU.max, op1=ALU.add, accum_out=tjunk[:, 0:1])
+            nc.vector.reciprocal(out=rx2[:, c0:c1], in_=tx[:, c0:c1])
 
-        rx_sq(0)
-        rx_sq(1)
-        rx_fin(0, 2)
-
-        gb = [bank(m, [P, P], F32, "gb") for m in range(NGRAM)]
-        kb = [None] * 8
-        for m in range(NGRAM, 8):
-            kb[m] = bank(m, [P, D], BF16, "kb")
-        for a in range(8):
-            ka = kraw[a // 2][:, a % 2, :]
-            for m in range(NGRAM):
-                nc.tensor.matmul(out=gb[m][:], lhsT=ka[:, m * P : (m + 1) * P], rhs=ka[:, m * P : (m + 1) * P], start=(a == 0), stop=(a == 7))
-            for m in range(NGRAM, 8):
-                nc.tensor.transpose(kb[m][:, a * P : (a + 1) * P], ka[:, m * P : (m + 1) * P], ident_b[:])
-        for m in range(NGRAM):
-            nc.vector.scalar_tensor_tensor(out=junk_v[:, 0:P], in0=gb[m][:], scalar=1.0, in1=ident_f[:], op0=ALU.mult, op1=ALU.mult, accum_out=ssk[:, m : m + 1])
-        nc.vector.tensor_copy(out=ktn[:, 5, :], in_=kb[5][:])
-        nc.vector.scalar_tensor_tensor(out=junk_v[:], in0=kb[5][:], scalar=1.0, in1=ktn[:, 5, :], op0=ALU.mult, op1=ALU.mult, accum_out=ssk[:, 5:6])
-        for m in (6, 7):
-            nc.scalar.activation(out=junk_s[:], in_=kb[m][:], func=ACT.Square, accum_out=ssk[:, cm(m) : cm(m) + 1])
-        nc.vector.scalar_tensor_tensor(out=rb[0][:], in0=pt[0][:], scalar=rx[:, 0:1], in1=rb[0][:], op0=ALU.mult, op1=ALU.mult)
-        nc.vector.tensor_scalar(out=tk[:], in0=ssk[:], scalar1=EPS, scalar2=-1.0, op0=ALU.max, op1=ALU.mult)
-        nc.vector.reciprocal(out=nrk2[:], in_=tk[:])
-        nc.scalar.activation(out=rk10[:], in_=nrk2[:], func=ACT.Sqrt, scale=-100.0)
-        rp = [bank(2, [P, H], F32, "rp"), bank(3, [P, H], F32, "rp")]
-        for m in range(8):
-            nc.tensor.matmul(out=rp[m // 4][:, (m % 4) * P : (m % 4 + 1) * P], lhsT=rk10[:, cm(m) : cm(m) + 1].to_broadcast([P, P]), rhs=ident_f[:], start=True, stop=True)
-        nc.scalar.copy(out=rkb[:, 0:H], in_=rp[0][:])
-        nc.vector.tensor_copy(out=rkb[:, H:C], in_=rp[1][:])
-        nc.vector.tensor_tensor(out=rb[0][:], in0=rb[0][:], in1=rkb[:], op=ALU.mult)
+        def rx_fin_s(c0, c1):
+            nc.scalar.activation(out=rx[:, c0:c1], in_=rx2[:, c0:c1], func=ACT.Sqrt)
+            nc.scalar.activation(out=nrx2[:, c0:c1], in_=rx2[:, c0:c1], func=ACT.Copy, scale=-1.0)
 
         def s_scale(r):
             nc.scalar.activation(out=rb[r][:], in_=rb[r][:], func=ACT.Copy, scale=rx[:, r : r + 1])
 
-        def g_mul(r):
-            nc.gpsimd.tensor_tensor(out=rb[r][:], in0=pt[r][:], in1=rb[r][:], op=ALU.mult)
-            nc.gpsimd.tensor_tensor(out=rb[r][:], in0=rb[r][:], in1=rkb[:], op=ALU.mult)
+        def g_mul1(r):
+            for n in range(GSPLIT):
+                cs = slice(C // GSPLIT * n, C // GSPLIT * (n + 1))
+                nc.gpsimd.tensor_tensor(out=rb[r][:, cs], in0=rb[r][:, cs], in1=pt[r][:, cs], op=ALU.mult)
 
-        s_scale(1)
-        g_mul(1)
-        for m in (6, 7):
-            nc.scalar.copy(out=ktn[:, m, :], in_=kb[m][:])
+        def g_mul2(r):
+            for n in range(GSPLIT):
+                cs = slice(C // GSPLIT * n, C // GSPLIT * (n + 1))
+                nc.gpsimd.tensor_tensor(out=rb[r][:, cs], in0=rb[r][:, cs], in1=rkb[:, cs], op=ALU.mult)
+
+        def g_mul(r):
+            g_mul1(r)
+            g_mul2(r)
+
+        def v_mul1(r):
+            nc.vector.scalar_tensor_tensor(out=rb[r][:], in0=pt[r][:], scalar=rx[:, r : r + 1], in1=rb[r][:], op0=ALU.mult, op1=ALU.mult)
+
+        def v_mul2(r):
+            nc.vector.tensor_tensor(out=rb[r][:], in0=rb[r][:], in1=rkb[:], op=ALU.mult)
 
         gps = [None] * NT
+        rp = []
         dz = [None] * NG
         dzg = [None] * NG
         xg = [None] * NG
-        tgp = [None] * NPAIR
+        tgp = [None] * (NPAIR + 2)
         tcd = [None] * NPAIR
         tsc = [None] * NPAIR
         aps = [None] * NT
@@ -218,15 +211,32 @@ def tile_rbf_softmax_layer_t_v_kernel(tc, x, kernel, rbf, probs, grad_out, out_0
                 dz[g] = dzpool.tile([P, J, C], BF16, name="dz", tag="dz")
             nc.vector.scalar_tensor_tensor(out=dz[g][:, r % J, :], in0=gps[r][:], scalar=s_all[:, r : r + 1], in1=rb[r][:], op0=ALU.subtract, op1=ALU.mult)
 
+        def op_w(r):
+            nc.vector.scalar_tensor_tensor(out=rb[r][:], in0=gps[r][:], scalar=s_all[:, r : r + 1], in1=rb[r][:], op0=ALU.subtract, op1=ALU.mult)
+
+        def op_f2(r):
+            g = r // J
+            if r % J == 0:
+                dz[g] = dzpool.tile([P, J, C], BF16, name="dz", tag="dz")
+            for n in range(2):
+                nc.vector.tensor_tensor(out=dz[g][:, r % J, H * n : H * n + H], in0=rb[r][:, H * n : H * n + H], in1=rp[n][:], op=ALU.mult)
+
+        def alloc_tgp(d):
+            tgp[d] = tgpool.tile([P, 2, 2, P, 4], BF16, name="tgp", tag="tgp", align_bytes=64)
+
+        tpss = {}
+
         def op_t(r):
-            d = r // 2
-            if r % 2 == 0:
-                tgp[d] = tgpool.tile([P, 2, 2, P, 4], BF16, name="tgp", tag="tgp", align_bytes=64)
             tps = bank(2 + r % 2, [P, 2, 2, P], F32, "tps")
+            tpss[r] = tps
             w = dz[r // J][:, r % J, :].bitcast(F32)
             for h in range(2):
                 for u in range(2):
                     nc.tensor.transpose(tps[:, h, u, :], w[:, 256 * h + u : 256 * (h + 1) : 2], ident_f[:])
+
+        def op_c(r):
+            d = r // 2
+            tps = tpss[r]
             dst = tgp[d][:, r % 2].rearrange("q h p t -> q (h p t)").bitcast(F32).rearrange("q (h p u) -> q h p u", h=2, u=2)
             nc.scalar.copy(out=dst, in_=tps[:].rearrange("q h u p -> q h p u"))
 
@@ -234,6 +244,11 @@ def tile_rbf_softmax_layer_t_v_kernel(tc, x, kernel, rbf, probs, grad_out, out_0
             tcd[d] = tcpool.tile([P, 4 * P], U32, name="tcd", tag="tcd", align_bytes=64)
             tsc[d] = tcpool.tile([P, 4 * P], U8, name="tsc", tag="tsc", align_bytes=64)
             nc.vector.quantize_mx(out=tcd[d][:].bitcast(E5), scales=tsc[d][:], in_=tgp[d][:].rearrange("q i h p t -> q (i h p t)"))
+            if RENDEZVOUS:
+                alloc_tgp(d + 2)
+                nc.gpsimd.memset(tgp[d + 2][:, 0, 0, 0:4, :], 0.0)
+            elif d + 2 < NPAIR:
+                alloc_tgp(d + 2)
 
         def op_mm(r):
             d = r // 2
@@ -257,31 +272,39 @@ def tile_rbf_softmax_layer_t_v_kernel(tc, x, kernel, rbf, probs, grad_out, out_0
                 nc.vector.scalar_tensor_tensor(out=junk_v[:, 0:H], in0=aps[r][n][:], scalar=nrx2[:, r : r + 1], in1=xr[r // J][:, r % J, H * n : H * n + H], op0=ALU.mult, op1=ALU.mult, accum_out=sg2[:, 2 * r + n : 2 * r + n + 1])
             nc.scalar.activation(out=sg[:, r : r + 1], in_=sg2[:, 2 * r : 2 * r + 1], func=ACT.Identity, bias=sg2[:, 2 * r + 1 : 2 * r + 2])
 
+        def loads_after(r):
+            if r + 6 < NT:
+                load_p(r + 6)
+                load_r(r + 6)
+
         def op_e0b(r):
             dx[r] = st.tile([P, D], F32, name="dx", tag="st")
             for n in range(2):
                 nc.vector.scalar_tensor_tensor(out=dx[r][:, H * n : H * n + H], in0=xr[r // J][:, r % J, H * n : H * n + H], scalar=sg[:, r : r + 1], in1=aps[r][n][:], op0=ALU.mult, op1=ALU.add)
             nc.sync.dma_start(out=o0_v[:, r // J, r % J, :], in_=dx[r][:])
 
-        def dzil(g):
-            dzg[g] = ilv.tile([P, C, J], BF16, name="dzg", tag="ilv", align_bytes=64)
-            for q in range(4):
-                ws = slice(256 * q, 256 * q + 256)
-                nc.scalar.copy(out=dzg[g][:, ws, :], in_=dz[g][:, :, ws].rearrange("p j w -> p w j"))
+        def dzil(g, q):
+            if q == 0:
+                dzg[g] = ilv.tile([P, C, J], BF16, name="dzg", tag="ilv", align_bytes=64)
+            ws = slice(256 * q, 256 * q + 256)
+            nc.scalar.copy(out=dzg[g][:, ws, :], in_=dz[g][:, :, ws].rearrange("p j w -> p w j"))
 
         def qd(g):
             nc.vector.quantize_mx(out=dzc[:, g, :].bitcast(E5), scales=dzs[:, g, :], in_=dzg[g][:].rearrange("p w j -> p (w j)"))
 
-        def xil(g):
-            xg[g] = ilv.tile([P, D, J], BF16, name="xg", tag="ilv", align_bytes=64)
-            for q in range(4):
-                ws = slice(256 * q, 256 * q + 256)
+        def xil(g, q, eng):
+            if q == 0:
+                xg[g] = ilv.tile([P, D, J], BF16, name="xg", tag="ilv", align_bytes=64)
+            ws = slice(256 * q, 256 * q + 256)
+            if eng == "G":
                 nc.gpsimd.tensor_scalar(out=xg[g][:, ws, :], in0=xr[g][:, :, ws].rearrange("p j w -> p w j"), scalar1=1.0, scalar2=0.0, op0=ALU.mult, op1=ALU.add)
+            else:
+                nc.scalar.copy(out=xg[g][:, ws, :], in_=xr[g][:, :, ws].rearrange("p j w -> p w j"))
 
         def qx(g):
             nc.vector.quantize_mx(out=xc[:, g, :].bitcast(E4), scales=xs[:, g, :], in_=xg[g][:].rearrange("p w j -> p (w j)"))
 
-        ring = [4, 5, 6, 7]
+        ring = [6, 7, 4, 5]
         ring_at = [0]
 
         def next_bank():
@@ -289,41 +312,58 @@ def tile_rbf_softmax_layer_t_v_kernel(tc, x, kernel, rbf, probs, grad_out, out_0
             ring_at[0] = ring_at[0] + 1
             return b
 
-        def ktg_half(h):
-            ktg = ilv.tile([P, D, 4], BF16, name="ktg", tag="ilv", align_bytes=64)
-            ktw = ktg[:].rearrange("q f t -> q (f t)").bitcast(F32)
-            for c in range(4):
-                tb = bank(next_bank(), [P, 2, 2, P], F32, "tb")
-                for a2 in range(2):
-                    kw = kraw[c][:, a2, :].bitcast(F32)
-                    for u in range(2):
-                        nc.tensor.transpose(tb[:, a2, u, :], kw[:, 256 * h + u : 256 * (h + 1) : 2], ident_f[:])
-                dst = ktw[:, 512 * c : 512 * c + 512].rearrange("q (a f u) -> q a f u", a=2, u=2)
+        ktg = [None] * 2
+
+        tbs = {}
+
+        def ktg_t(h, c):
+            tb = bank(next_bank(), [P, 2, 2, P], F32, "tb")
+            tbs[(h, c)] = tb
+            for a2 in range(2):
+                kw = kraw[c][:, a2, :].bitcast(F32)
+                for u in range(2):
+                    nc.tensor.transpose(tb[:, a2, u, :], kw[:, 256 * h + u : 256 * (h + 1) : 2], ident_f[:])
+
+        def ktg_c(h, c, eng):
+            if c == 0:
+                ktg[h] = ilv.tile([P, D, 4], BF16, name="ktg", tag="ilv", align_bytes=64)
+            ktw = ktg[h][:].rearrange("q f t -> q (f t)").bitcast(F32)
+            tb = tbs[(h, c)]
+            dst = ktw[:, 512 * c : 512 * c + 512].rearrange("q (a f u) -> q a f u", a=2, u=2)
+            if eng == "V":
                 nc.vector.tensor_copy(out=dst, in_=tb[:].rearrange("q a u f -> q a f u"))
-            nc.vector.quantize_mx(out=ktc[:, h, :].bitcast(E4), scales=kts[:, h, :], in_=ktg[:].rearrange("q f t -> q (f t)"))
+            else:
+                nc.scalar.copy(out=dst, in_=tb[:].rearrange("q a u f -> q a f u"))
 
-        def ktn_block(m):
-            kbm = bank(next_bank(), [P, D], BF16, "kb")
+        def s_item(it):
+            if it[0] == "rx":
+                rx_sq(it[1])
+            if it[0] == "xil":
+                xil(it[1], it[2], "S")
+            if it[0] == "dzil":
+                dzil(it[1], it[2])
+
+        def ktg_q(h):
+            nc.vector.quantize_mx(out=ktc[:, h, :].bitcast(E4), scales=kts[:, h, :], in_=ktg[h][:].rearrange("q f t -> q (f t)"))
+
+        kbs = {}
+
+        def ktn_t(m):
+            kbs[m] = bank(next_bank(), [P, D], BF16, "kb")
             for a in range(8):
-                nc.tensor.transpose(kbm[:, a * P : (a + 1) * P], kraw[a // 2][:, a % 2, m * P : (m + 1) * P], ident_b[:])
-            nc.vector.tensor_copy(out=ktn[:, m, :], in_=kbm[:])
+                nc.tensor.transpose(kbs[m][:, a * P : (a + 1) * P], kraw[a // 2][:, a % 2, m * P : (m + 1) * P], ident_b[:])
 
-        gcopy(0)
-        gcopy(1)
-        rx_sq(2)
-        rx_sq(3)
-        rx_fin(2, 4)
-        s_scale(2)
-        g_mul(2)
-        s_scale(3)
-        g_mul(3)
+        def ktn_c(m, eng):
+            kbm = kbs[m]
+            if eng == "V":
+                nc.vector.tensor_copy(out=ktn[:, m, :], in_=kbm[:])
+            else:
+                nc.scalar.copy(out=ktn[:, m, :], in_=kbm[:])
 
-        cbanks = [(0, 1), (2, 3), (4, 5)]
         cps = [None] * 8
         dk = [None] * 8
 
-        def c_alloc(m):
-            b = cbanks[m % 3]
+        def c_alloc(m, b):
             cps[m] = [bank(b[0], [P, H], F32, "cps"), bank(b[1], [P, H], F32, "cps")]
 
         def c_mm(m, gs):
@@ -339,81 +379,24 @@ def tile_rbf_softmax_layer_t_v_kernel(tc, x, kernel, rbf, probs, grad_out, out_0
                         stop=(g == NG - 1),
                     )
 
-        for d in range(NPAIR + 2):
-            e = d - 2
-            if e >= 0:
-                op_e0a(2 * e)
-                op_e0a(2 * e + 1)
-                op_e0b(2 * e)
-                op_e0b(2 * e + 1)
-            if d == 0:
-                ktg_half(0)
-                ktg_half(1)
-            if d == 1:
-                for m in range(NGRAM):
-                    ktn_block(m)
-            if 1 <= d <= NPAIR:
-                op_q(d - 1)
-                op_mm(2 * d - 2)
-                op_mm(2 * d - 1)
-            if d == 7:
-                qd(2)
-                qx(2)
-            if d == 0:
-                for r in range(4, 8):
-                    rx_sq(r)
-                rx_fin(4, 8)
-            if d == 2:
-                for r in range(8, 12):
-                    rx_sq(r)
-                rx_fin(8, 12)
-            for r in (2 * d + 4, 2 * d + 5):
-                if r < NT:
-                    s_scale(r)
-                    g_mul(r)
-            if d == 6:
-                qx(0)
-                qx(1)
-            if d in (2, 4, 6):
-                dzil(d // 2 - 1)
-            if d in (4, 5, 6):
-                xil(d - 4)
-            if d == 6:
-                c_alloc(0)
-                c_mm(0, (0, 1))
-                c_alloc(1)
-                c_mm(1, (0, 1))
-            if d < NPAIR:
-                op_a(2 * d)
-                op_a(2 * d + 1)
-                for r in (2 * d, 2 * d + 1):
-                    if r + 6 < NT:
-                        load_p(r + 6)
-                for r in (2 * d, 2 * d + 1):
-                    op_f(r)
-                    if r + 6 < NT:
-                        load_r(r + 6)
-                    op_t(r)
-                if d + 1 < NPAIR:
-                    if d == 1:
-                        alloc_g(2)
-                        load_g(2, 0, 4)
-                    gcopy(2 * d + 2)
-                    gcopy(2 * d + 3)
-            if d in (3, 5):
-                qd(d // 2 - 1)
+        def e1a(m, n):
+            nc.vector.scalar_tensor_tensor(out=junk_v[:, 0:H], in0=cps[m][n][:], scalar=nrk2[:, cm(m) : cm(m) + 1], in1=ktn[:, m, H * n : H * n + H], op0=ALU.mult, op1=ALU.mult, accum_out=cg2[:, 2 * m + n : 2 * m + n + 1])
 
-        def e1a(m):
-            for n in range(2):
-                nc.vector.scalar_tensor_tensor(out=junk_v[:, 0:H], in0=cps[m][n][:], scalar=nrk2[:, cm(m) : cm(m) + 1], in1=ktn[:, m, H * n : H * n + H], op0=ALU.mult, op1=ALU.mult, accum_out=cg2[:, 2 * m + n : 2 * m + n + 1])
-            nc.scalar.activation(out=cg[:, m : m + 1], in_=cg2[:, 2 * m : 2 * m + 1], func=ACT.Identity, bias=cg2[:, 2 * m + 1 : 2 * m + 2])
+        def e1s(m):
+            nc.vector.tensor_tensor(out=cg[:, m : m + 1], in0=cg2[:, 2 * m : 2 * m + 1], in1=cg2[:, 2 * m + 1 : 2 * m + 2], op=ALU.add)
 
-        def e1b(m):
-            dk[m] = st.tile([P, D], F32, name="dk", tag="st")
-            for n in range(2):
-                nc.vector.scalar_tensor_tensor(out=dk[m][:, H * n : H * n + H], in0=ktn[:, m, H * n : H * n + H], scalar=cg[:, m : m + 1], in1=cps[m][n][:], op0=ALU.mult, op1=ALU.add)
-            o1s = st.tile([P, 8, P], F32, name="o1s", tag="st")
-            for hf in range(2):
+        def e1b(m, n):
+            if n == 0:
+                dk[m] = ppool.tile([P, D], F32, name="dk", tag="pt")
+            nc.vector.scalar_tensor_tensor(out=dk[m][:, H * n : H * n + H], in0=ktn[:, m, H * n : H * n + H], scalar=cg[:, m : m + 1], in1=cps[m][n][:], op0=ALU.mult, op1=ALU.add)
+
+        o1 = {}
+
+        def e1c(m, hfs):
+            if hfs[0] == 0:
+                o1[m] = rpool.tile([P, 8, P], F32, name="o1s", tag="rb")
+            o1s = o1[m]
+            for hf in hfs:
                 bt = bank(6 + hf, [P, 4, P], F32, "bt")
                 for a in range(4):
                     nc.tensor.transpose(bt[:, a, :], dk[m][:, P * (4 * hf + a) : P * (4 * hf + a) + P], ident_f[:])
@@ -421,15 +404,225 @@ def tile_rbf_softmax_layer_t_v_kernel(tc, x, kernel, rbf, probs, grad_out, out_0
                     nc.vector.tensor_copy(out=o1s[:, 4 * hf : 4 * hf + 4, :], in_=bt[:])
                 else:
                     nc.scalar.copy(out=o1s[:, 4 * hf : 4 * hf + 4, :], in_=bt[:])
-            nc.sync.dma_start(out=o1_v[:, :, P * m : P * m + P], in_=o1s[:])
+                if m == 7:
+                    nc.sync.dma_start(out=o1_v[:, 4 * hf : 4 * hf + 4, P * m : P * m + P], in_=o1s[:, 4 * hf : 4 * hf + 4, :])
+            if m < 7:
+                nc.sync.dma_start(out=o1_v[:, :, P * m : P * m + P], in_=o1s[:])
 
+
+        sgs = keep.tile([P, 16], F32, name="sgs")
+        gp_a = {}
+        gp_p = {}
+
+        def gp_copy(key, ps):
+            gp_a[key] = ppool.tile([P, D], F32, name="gpa", tag="pt")
+            for n in range(2):
+                nc.scalar.copy(out=gp_a[key][:, H * n : H * n + H], in_=ps[n][:])
+
+        def gp_prod(key, opnd):
+            gp_p[key] = rpool.tile([P, D], F32, name="gpp", tag="rb")
+            nc.gpsimd.tensor_tensor(out=gp_p[key][:], in0=gp_a[key][:], in1=opnd, op=ALU.mult)
+
+        def gp_sum(key, col, nr2):
+            nc.scalar.activation(out=junk_s[:], in_=gp_p[key][:], func=ACT.Copy, scale=nr2, accum_out=sgs[:, col : col + 1])
+
+        def gp_fin(key, col, opnd, out):
+            nc.gpsimd.tensor_scalar(out=gp_p[key][:], in0=opnd, scalar1=sgs[:, col : col + 1], scalar2=0.0, op0=ALU.mult, op1=ALU.add)
+            nc.gpsimd.tensor_tensor(out=out, in0=gp_p[key][:], in1=gp_a[key][:], op=ALU.add)
+
+        def x_row(r):
+            return xr[r // J][:, r % J, :]
+
+        gb = [bank(m, [P, P], F32, "gb") for m in range(NGRAM)]
+        kb = [None] * 8
+        for m in range(NGRAM, 8):
+            kb[m] = bank(m, [P, D], BF16, "kb")
+        for a in range(8):
+            ka = kraw[a // 2][:, a % 2, :]
+            for m in range(NGRAM):
+                nc.tensor.matmul(out=gb[m][:], lhsT=ka[:, m * P : (m + 1) * P], rhs=ka[:, m * P : (m + 1) * P], start=(a == 0), stop=(a == 7))
+            for m in range(NGRAM, 8):
+                nc.tensor.transpose(kb[m][:, a * P : (a + 1) * P], ka[:, m * P : (m + 1) * P], ident_b[:])
+        rx_sq(0)
+        rx_sq(1)
+        nc.scalar.activation(out=junk_s[:], in_=kb[6][:], func=ACT.Square, accum_out=ssk[:, cm(6) : cm(6) + 1])
+        for m in range(NGRAM):
+            nc.vector.scalar_tensor_tensor(out=junk_v[:, 0:P], in0=gb[m][:], scalar=1.0, in1=ident_f[:], op0=ALU.mult, op1=ALU.mult, accum_out=ssk[:, m : m + 1])
+        rx_fin_v(0, 2)
+        rx_fin_s(0, 2)
+        nc.scalar.activation(out=junk_s[:], in_=kb[7][:], func=ACT.Square, accum_out=ssk[:, cm(7) : cm(7) + 1])
+        gcopy(0)
+        gcopy(1)
+        v_mul1(0)
+        for m in range(NGRAM, 8):
+            nc.scalar.copy(out=ktn[:, m, :], in_=kb[m][:])
+        op_a(0)
+        nc.vector.tensor_scalar(out=tk[:], in0=ssk[:], scalar1=EPS, scalar2=None, op0=ALU.max, op1=ALU.add, accum_out=tjunk[:, 1:2])
+        nc.vector.reciprocal(out=rk2[:], in_=tk[:])
+        nc.scalar.activation(out=rk10[:], in_=rk2[:], func=ACT.Sqrt, scale=100.0)
+        nc.scalar.activation(out=nrk2[:], in_=rk2[:], func=ACT.Copy, scale=-1.0)
+        ktg_t(0, 0)
+        ktg_t(0, 1)
+        rp.append(bank(4, [P, H], F32, "rp"))
+        rp.append(bank(5, [P, H], F32, "rp"))
+        for m in range(8):
+            nc.tensor.transpose(rp[m // 4][:, (m % 4) * P : (m % 4 + 1) * P], rk10[:, cm(m) : cm(m) + 1].to_broadcast([P, P]), ident_f[:])
+        v_mul1(1)
+        op_w(0)
+        nc.scalar.copy(out=rkb[:, 0:H], in_=rp[0][:])
+        nc.scalar.copy(out=rkb[:, H:C], in_=rp[1][:])
+        op_a(1)
+        g_mul(2)
+        alloc_tgp(0)
+        alloc_tgp(1)
+        gcopy(2)
+        op_f2(0)
+        loads_after(0)
+        op_t(0)
+        rx_sq(2)
+        rx_sq(3)
+        op_w(1)
+        gcopy(3)
+        op_f2(1)
+        loads_after(1)
+        op_t(1)
+        op_c(0)
+        rx_fin_v(2, 4)
+        rx_fin_s(2, 4)
+        g_mul(3)
+        s_scale(2)
+        ktg_t(0, 2)
+        ktg_t(0, 3)
+        op_a(2)
+        op_a(3)
+        rx_sq(4)
+        op_c(1)
+        rx_sq(5)
+        rx_sq(6)
+        op_f(2)
+        loads_after(2)
+        op_t(2)
+        g_mul(4)
+        for c in range(4):
+            ktg_c(0, c, "V")
+            ktg_t(1, c)
+        s_scale(3)
+        op_c(2)
+        rx_sq(7)
+        ktg_q(0)
+        op_f(3)
+        loads_after(3)
+        alloc_g(2)
+        load_g(2, 0, 4)
+        gcopy(4)
+        op_t(3)
+        gcopy(5)
+        for c in range(3):
+            ktg_c(1, c, "S")
+            ktn_t(c)
+        op_c(3)
+        ktg_c(1, 3, "S")
+        ktn_t(3)
+        op_q(0)
+        g_mul(5)
+        rx_fin_v(4, 8)
+        rx_fin_s(4, 8)
+        op_a(4)
+        op_a(5)
+        for m in range(4):
+            ktn_c(m, "S")
+            if m + 4 < NGRAM:
+                ktn_t(m + 4)
+        for m in range(4, NGRAM):
+            ktn_c(m, "S")
+        ktg_q(1)
+        op_q(1)
+        op_mm(0)
+        op_mm(1)
+        for r in range(6, 6 + 2 * (GLEAD - 1)):
+            g_mul(r)
+
+        for d in range(2, NPAIR + 2):
+            e = d - 2
+            op_e0a(2 * e)
+            op_e0a(2 * e + 1)
+            if d == 4:
+                rx_fin_v(8, 12)
+                rx_fin_s(8, 12)
+            if d in (3, 5):
+                qd(d // 2 - 1)
+            if d == 6:
+                qx(0)
+            if d == 7:
+                qx(1)
+                qd(2)
+            if 3 <= d <= NPAIR:
+                op_q(d - 1)
+            op_e0b(2 * e)
+            op_e0b(2 * e + 1)
+            if d <= NPAIR:
+                op_mm(2 * d - 2)
+                op_mm(2 * d - 1)
+            if d == 7:
+                qx(2)
+            for r in (2 * d + 2 * GLEAD, 2 * d + 2 * GLEAD + 1):
+                if r < NT:
+                    g_mul(r)
+            if d in (4, 5, 6):
+                for q in range(4):
+                    xil(d - 4, q, "G")
+            if d in (2, 4, 6):
+                dzil(d // 2 - 1, 0)
+            if d < NPAIR:
+                s_scale(2 * d)
+                s_scale(2 * d + 1)
+            if d in (2, 4, 6):
+                for q in range(1, 4):
+                    dzil(d // 2 - 1, q)
+            if d == 3:
+                for r in range(8, 12):
+                    rx_sq(r)
+            if d == 7:
+                c_alloc(0, (0, 1))
+                c_mm(0, (0, 1))
+                c_alloc(1, (2, 3))
+                c_mm(1, (0, 1))
+            if d < NPAIR:
+                if d > 2:
+                    op_a(2 * d)
+                    op_a(2 * d + 1)
+                for r in (2 * d, 2 * d + 1):
+                    op_f(r)
+                    loads_after(r)
+                    op_t(r)
+                    op_c(r)
+                if d + 1 < NPAIR:
+                    gcopy(2 * d + 2)
+                    gcopy(2 * d + 3)
+
+        ALLG = (0, 1, 2)
+        vb = [(0, 1), (2, 3), (4, 5)]
         c_mm(0, (2,))
         c_mm(1, (2,))
-        e1a(0)
+        c_alloc(2, vb[2])
+        c_mm(2, ALLG)
+        e1a(0, 0)
+        e1a(0, 1)
         for m in range(8):
-            if m + 2 < 8:
-                c_alloc(m + 2)
-                c_mm(m + 2, (0, 1, 2))
             if m + 1 < 8:
-                e1a(m + 1)
-            e1b(m)
+                e1a(m + 1, 0)
+            e1s(m)
+            if m + 1 < 8:
+                e1a(m + 1, 1)
+            if m < 7:
+                e1b(m, 0)
+                e1b(m, 1)
+                if m + 3 < 8:
+                    c_alloc(m + 3, vb[(m + 3) % 3])
+                    c_mm(m + 3, ALLG)
+                e1c(m, (0, 1))
+            else:
+                e1b(m, 0)
+                e1c(m, (0,))
+                e1b(m, 1)
+                e1c(m, (1,))

@@ -30,6 +30,7 @@ KTN_ENG = "S"
 XIL_S = False
 GSPLIT = 1
 GLEAD = 2
+NGK = 0
 RENDEZVOUS = True
 V_MUL = (0, 1)
 GP_E0 = ()
@@ -250,9 +251,10 @@ def tile_rbf_softmax_layer_t_v_kernel(tc, x, kernel, rbf, probs, grad_out, out_0
             elif d + 2 < NPAIR:
                 alloc_tgp(d + 2)
 
-        def op_mm(r):
+        def op_mm(r, b0=None):
             d = r // 2
-            b0 = 4 + 2 * (r % 2)
+            if b0 is None:
+                b0 = 4 + 2 * (r % 2)
             aps[r] = [bank(b0, [P, H], F32, "aps"), bank(b0 + 1, [P, H], F32, "aps")]
             for n in range(2):
                 for h in range(2):
@@ -270,6 +272,8 @@ def tile_rbf_softmax_layer_t_v_kernel(tc, x, kernel, rbf, probs, grad_out, out_0
         def op_e0a(r):
             for n in range(2):
                 nc.vector.scalar_tensor_tensor(out=junk_v[:, 0:H], in0=aps[r][n][:], scalar=nrx2[:, r : r + 1], in1=xr[r // J][:, r % J, H * n : H * n + H], op0=ALU.mult, op1=ALU.mult, accum_out=sg2[:, 2 * r + n : 2 * r + n + 1])
+            if r >= 11:
+                return
             nc.scalar.activation(out=sg[:, r : r + 1], in_=sg2[:, 2 * r : 2 * r + 1], func=ACT.Identity, bias=sg2[:, 2 * r + 1 : 2 * r + 2])
 
         def loads_after(r):
@@ -280,14 +284,21 @@ def tile_rbf_softmax_layer_t_v_kernel(tc, x, kernel, rbf, probs, grad_out, out_0
         def op_e0b(r):
             dx[r] = st.tile([P, D], F32, name="dx", tag="st")
             for n in range(2):
-                nc.vector.scalar_tensor_tensor(out=dx[r][:, H * n : H * n + H], in0=xr[r // J][:, r % J, H * n : H * n + H], scalar=sg[:, r : r + 1], in1=aps[r][n][:], op0=ALU.mult, op1=ALU.add)
-            nc.sync.dma_start(out=o0_v[:, r // J, r % J, :], in_=dx[r][:])
+                nc.vector.scalar_tensor_tensor(out=dx[r][:, H * n : H * n + H], in0=xr[r // J][:, r % J, H * n : H * n + H], scalar=(sg[:, r : r + 1] if r < 10 else sgv[:, r - 10 : r - 9]), in1=aps[r][n][:], op0=ALU.mult, op1=ALU.add)
+                if r == NT - 1:
+                    nc.sync.dma_start(out=o0_v[:, r // J, r % J, H * n : H * n + H], in_=dx[r][:, H * n : H * n + H])
+            if r < NT - 1:
+                nc.sync.dma_start(out=o0_v[:, r // J, r % J, :], in_=dx[r][:])
 
         def dzil(g, q):
             if q == 0:
                 dzg[g] = ilv.tile([P, C, J], BF16, name="dzg", tag="ilv", align_bytes=64)
             ws = slice(256 * q, 256 * q + 256)
             nc.scalar.copy(out=dzg[g][:, ws, :], in_=dz[g][:, :, ws].rearrange("p j w -> p w j"))
+
+        def dzil_g(g, q):
+            ws = slice(256 * q, 256 * q + 256)
+            nc.gpsimd.tensor_scalar(out=dzg[g][:, ws, :], in0=dz[g][:, :, ws].rearrange("p j w -> p w j"), scalar1=1.0, scalar2=0.0, op0=ALU.mult, op1=ALU.add)
 
         def qd(g):
             nc.vector.quantize_mx(out=dzc[:, g, :].bitcast(E5), scales=dzs[:, g, :], in_=dzg[g][:].rearrange("p w j -> p (w j)"))
@@ -387,7 +398,7 @@ def tile_rbf_softmax_layer_t_v_kernel(tc, x, kernel, rbf, probs, grad_out, out_0
 
         def e1b(m, n):
             if n == 0:
-                dk[m] = ppool.tile([P, D], F32, name="dk", tag="pt")
+                dk[m] = st.tile([P, D], F32, name="dk", tag="st")
             nc.vector.scalar_tensor_tensor(out=dk[m][:, H * n : H * n + H], in0=ktn[:, m, H * n : H * n + H], scalar=cg[:, m : m + 1], in1=cps[m][n][:], op0=ALU.mult, op1=ALU.add)
 
         o1 = {}
@@ -397,20 +408,20 @@ def tile_rbf_softmax_layer_t_v_kernel(tc, x, kernel, rbf, probs, grad_out, out_0
                 o1[m] = rpool.tile([P, 8, P], F32, name="o1s", tag="rb")
             o1s = o1[m]
             for hf in hfs:
-                bt = bank(6 + hf, [P, 4, P], F32, "bt")
+                bt = bank((6 if m < 6 else (4 if m == 6 else 0)) + hf, [P, 4, P], F32, "bt")
                 for a in range(4):
                     nc.tensor.transpose(bt[:, a, :], dk[m][:, P * (4 * hf + a) : P * (4 * hf + a) + P], ident_f[:])
-                if m == 7 and hf == 1:
+                if m == 7:
                     nc.vector.tensor_copy(out=o1s[:, 4 * hf : 4 * hf + 4, :], in_=bt[:])
+                    nc.sync.dma_start(out=o1_v[:, 4 * hf : 4 * hf + 4, P * m : P * m + P], in_=o1s[:, 4 * hf : 4 * hf + 4, :])
                 else:
                     nc.scalar.copy(out=o1s[:, 4 * hf : 4 * hf + 4, :], in_=bt[:])
-                if m == 7:
-                    nc.sync.dma_start(out=o1_v[:, 4 * hf : 4 * hf + 4, P * m : P * m + P], in_=o1s[:, 4 * hf : 4 * hf + 4, :])
             if m < 7:
-                nc.sync.dma_start(out=o1_v[:, :, P * m : P * m + P], in_=o1s[:])
+                nc.scalar.dma_start(out=o1_v[:, :, P * m : P * m + P], in_=o1s[:])
 
 
         sgs = keep.tile([P, 16], F32, name="sgs")
+        sgv = keep.tile([P, 8], F32, name="sgv")
         gp_a = {}
         gp_p = {}
 
@@ -542,7 +553,7 @@ def tile_rbf_softmax_layer_t_v_kernel(tc, x, kernel, rbf, probs, grad_out, out_0
         for r in range(6, 6 + 2 * (GLEAD - 1)):
             g_mul(r)
 
-        for d in range(2, NPAIR + 2):
+        for d in range(2, NPAIR):
             e = d - 2
             op_e0a(2 * e)
             op_e0a(2 * e + 1)
@@ -553,22 +564,17 @@ def tile_rbf_softmax_layer_t_v_kernel(tc, x, kernel, rbf, probs, grad_out, out_0
                 qd(d // 2 - 1)
             if d == 6:
                 qx(0)
-            if d == 7:
-                qx(1)
-                qd(2)
             if 3 <= d <= NPAIR:
                 op_q(d - 1)
             op_e0b(2 * e)
             op_e0b(2 * e + 1)
-            if d <= NPAIR:
+            if d < NPAIR:
                 op_mm(2 * d - 2)
                 op_mm(2 * d - 1)
-            if d == 7:
-                qx(2)
             for r in (2 * d + 2 * GLEAD, 2 * d + 2 * GLEAD + 1):
                 if r < NT:
                     g_mul(r)
-            if d in (4, 5, 6):
+            if d in (4, 5):
                 for q in range(4):
                     xil(d - 4, q, "G")
             if d in (2, 4, 6):
@@ -582,11 +588,9 @@ def tile_rbf_softmax_layer_t_v_kernel(tc, x, kernel, rbf, probs, grad_out, out_0
             if d == 3:
                 for r in range(8, 12):
                     rx_sq(r)
-            if d == 7:
-                c_alloc(0, (0, 1))
-                c_mm(0, (0, 1))
-                c_alloc(1, (2, 3))
-                c_mm(1, (0, 1))
+            if d == 5:
+                for q in range(4):
+                    xil(2, q, "S")
             if d < NPAIR:
                 if d > 2:
                     op_a(2 * d)
@@ -600,29 +604,82 @@ def tile_rbf_softmax_layer_t_v_kernel(tc, x, kernel, rbf, probs, grad_out, out_0
                     gcopy(2 * d + 2)
                     gcopy(2 * d + 3)
 
+        def k_row(m):
+            return ktn[:, m, :]
+
+        def gx_fin(t):
+            dx[t] = st.tile([P, D], F32, name="dx", tag="st")
+            gp_fin(("x", t), t, x_row(t), dx[t][:])
+            nc.sync.dma_start(out=o0_v[:, t // J, t % J, :], in_=dx[t][:])
+
+        def gk_fin(m):
+            dk[m] = st.tile([P, D], F32, name="dk", tag="st")
+            gp_fin(("k", m), 12 + m, k_row(m), dk[m][:])
+
         ALLG = (0, 1, 2)
         vb = [(0, 1), (2, 3), (4, 5)]
-        c_mm(0, (2,))
-        c_mm(1, (2,))
+        dzil(2, 0)
+        dzil_g(2, 2)
+        dzil(2, 1)
+        dzil_g(2, 3)
+        op_e0a(8)
+        op_e0a(9)
+        qx(0)
+        op_q(5)
+        op_e0b(8)
+        op_e0b(9)
+        op_mm(10, 4)
+        op_mm(11, 6)
+        qx(1)
+        gp_copy(("x", 10), aps[10])
+        gp_copy(("x", 11), aps[11])
+        gp_prod(("x", 10), x_row(10))
+        gp_prod(("x", 11), x_row(11))
+        c_alloc(0, vb[0])
+        c_mm(0, (0, 1))
+        c_alloc(1, vb[1])
+        c_mm(1, (0, 1))
         c_alloc(2, vb[2])
-        c_mm(2, ALLG)
-        e1a(0, 0)
-        e1a(0, 1)
-        for m in range(8):
+        c_mm(2, (0, 1))
+        qd(2)
+        qx(2)
+        gp_sum(("x", 10), 10, nrx2[:, 10:11])
+        gp_sum(("x", 11), 11, nrx2[:, 11:12])
+        first_v = NGK
+        c_mm(first_v, (2,))
+        for m in range(3):
+            if m != first_v:
+                c_mm(m, (2,))
+        for m in range(NGK):
+            gp_copy(("k", m), cps[m])
+            c_alloc(m + 3, vb[m % 3])
+            c_mm(m + 3, ALLG)
+        if NGK > 0:
+            gp_prod(("k", 0), k_row(0))
+        gx_fin(10)
+        gx_fin(11)
+        if NGK > 0:
+            gp_sum(("k", 0), 12, nrk2[:, cm(0) : cm(0) + 1])
+        if NGK > 1:
+            gp_prod(("k", 1), k_row(1))
+            gp_sum(("k", 1), 13, nrk2[:, cm(1) : cm(1) + 1])
+        for m in range(NGK):
+            gk_fin(m)
+        e1a(first_v, 0)
+        e1a(first_v, 1)
+        for m in range(first_v, 8):
             if m + 1 < 8:
                 e1a(m + 1, 0)
             e1s(m)
             if m + 1 < 8:
                 e1a(m + 1, 1)
-            if m < 7:
-                e1b(m, 0)
-                e1b(m, 1)
-                if m + 3 < 8:
-                    c_alloc(m + 3, vb[(m + 3) % 3])
-                    c_mm(m + 3, ALLG)
-                e1c(m, (0, 1))
-            else:
-                e1b(m, 0)
-                e1c(m, (0,))
-                e1b(m, 1)
-                e1c(m, (1,))
+            e1b(m, 0)
+            e1b(m, 1)
+            if m + 3 < 8:
+                c_alloc(m + 3, vb[(m + 3) % 3])
+                c_mm(m + 3, ALLG)
+            e1c(m, (0, 1))
+            if m == 4 and NGK > 0:
+                e1c(0, (0, 1))
+            if m == 6 and NGK > 1:
+                e1c(1, (0, 1))

@@ -31,6 +31,9 @@ XIL_S = False
 GSPLIT = 1
 GLEAD = 2
 NGK = 0
+W_HEAD = 0
+W_MID = 5
+W_END = 6
 RENDEZVOUS = True
 V_MUL = (0, 1)
 GP_E0 = ()
@@ -197,6 +200,12 @@ def tile_rbf_softmax_layer_t_v_kernel(tc, x, kernel, rbf, probs, grad_out, out_0
         tsc = [None] * NPAIR
         aps = [None] * NT
         dx = [None] * NT
+
+        def warm(n, b, d):
+            if n > 0:
+                wps = bank(b, [P, H], F32, "wps")
+                for k in range(n):
+                    nc.tensor.matmul_mx(out=wps[:], lhsT=tcd[d][:, 0:P].bitcast(E5), lhsT_scale=tsc[d][:, 0:P], rhs=ktc[:, 0, 0:H].bitcast(E4), rhs_scale=kts[:, 0, 0:H], start=True, stop=True)
 
         def gcopy(r):
             gps[r] = bank(r % 2, [P, C], BF16, "gps")
@@ -571,6 +580,7 @@ def tile_rbf_softmax_layer_t_v_kernel(tc, x, kernel, rbf, probs, grad_out, out_0
             if d < NPAIR:
                 op_mm(2 * d - 2)
                 op_mm(2 * d - 1)
+                warm(W_MID, 2, d - 1)
             for r in (2 * d + 2 * GLEAD, 2 * d + 2 * GLEAD + 1):
                 if r < NT:
                     g_mul(r)
@@ -603,6 +613,8 @@ def tile_rbf_softmax_layer_t_v_kernel(tc, x, kernel, rbf, probs, grad_out, out_0
                 if d + 1 < NPAIR:
                     gcopy(2 * d + 2)
                     gcopy(2 * d + 3)
+                warm(W_END, 2, d - 1)
+                warm(W_END, 3, d - 1)
 
         def k_row(m):
             return ktn[:, m, :]

@@ -16,30 +16,19 @@ ALU = mybir.AluOpType
 ACT = mybir.ActivationFunctionType
 
 P = 128
-NG = 3
 J = 4
+NG = B // (P * J)
 NT = NG * J
 NPAIR = NT // 2
 H = 512
+NH = C // H
+NB = C // P
+PIECE = 256
+WORDS = H // 2
+RING = 6
+NCHUNK = 4
 EPS = 1e-12
 NGRAM = 6
-
-MANUAL = True
-KTG_ENG = "S"
-KTN_ENG = "S"
-XIL_S = False
-GSPLIT = 1
-GLEAD = 2
-NGK = 0
-W_HEAD = 0
-W_MID = 5
-W_END = 6
-RENDEZVOUS = True
-V_MUL = (0, 1)
-GP_E0 = ()
-GPC = False
-C_G = (0,)
-C_V = (1, 2, 3, 4, 5, 6, 7)
 
 
 def tile_rbf_softmax_layer_t_v_kernel(tc, x, kernel, rbf, probs, grad_out, out_0, out_1):
@@ -57,17 +46,17 @@ def tile_rbf_softmax_layer_t_v_kernel(tc, x, kernel, rbf, probs, grad_out, out_0
         st = ctx.enter_context(tc.tile_pool(name="st", bufs=6))
         ilv = ctx.enter_context(tc.tile_pool(name="ilv", bufs=3))
         gpool = ctx.enter_context(tc.tile_pool(name="gpool", bufs=2))
-        ppool = ctx.enter_context(tc.tile_pool(name="ppool", bufs=6))
-        rpool = ctx.enter_context(tc.tile_pool(name="rpool", bufs=6))
+        ppool = ctx.enter_context(tc.tile_pool(name="ppool", bufs=RING))
+        rpool = ctx.enter_context(tc.tile_pool(name="rpool", bufs=RING))
         dzpool = ctx.enter_context(tc.tile_pool(name="dzpool", bufs=2))
         tgpool = ctx.enter_context(tc.tile_pool(name="tgpool", bufs=2))
         tcpool = ctx.enter_context(tc.tile_pool(name="tcpool", bufs=2))
         psum = ctx.enter_context(tc.psum_pool(name="psum", bufs=1))
-        if MANUAL:
-            ctx.enter_context(tc.manual_schedule())
+        ctx.enter_context(tc.manual_schedule())
 
         def bank(b, shape, dtype, nm):
             return psum.tile(shape, dtype, name="%s_b%d" % (nm, b), tag="b%d" % b)
+
 
         one = keep.tile([P, 1], F32, name="one")
         nc.vector.memset(one[:], 1.0)
@@ -81,9 +70,9 @@ def tile_rbf_softmax_layer_t_v_kernel(tc, x, kernel, rbf, probs, grad_out, out_0
         junk_v = keep.tile([P, C], F32, name="junk_v")
         junk_s = keep.tile([P, C], BF16, name="junk_s")
 
-        ktn = keep.tile([P, 8, D], BF16, name="ktn")
-        ktc = keep.tile([P, 2, D], U32, name="ktc", align_bytes=64)
-        kts = keep.tile([P, 2, D], U8, name="kts", align_bytes=64)
+        ktn = keep.tile([P, NB, D], BF16, name="ktn")
+        ktc = keep.tile([P, NH, D], U32, name="ktc", align_bytes=64)
+        kts = keep.tile([P, NH, D], U8, name="kts", align_bytes=64)
         xc = keep.tile([P, NG, D], U32, name="xc", align_bytes=64)
         xs = keep.tile([P, NG, D], U8, name="xs", align_bytes=64)
         dzc = keep.tile([P, NG, C], U32, name="dzc", align_bytes=64)
@@ -106,16 +95,18 @@ def tile_rbf_softmax_layer_t_v_kernel(tc, x, kernel, rbf, probs, grad_out, out_0
         sg = keep.tile([P, NT], F32, name="sg")
         cg2 = keep.tile([P, 16], F32, name="cg2")
         cg = keep.tile([P, 8], F32, name="cg")
+        sgs = keep.tile([P, 16], F32, name="sgs")
 
         nc.vector.memset(ssk[:], 1.0)
 
-        def cm(m):
-            return m if m < 6 else m + 2
+        def kcol(m):
+            return m if m < NGRAM else m + 2
 
         xr = [keep.tile([P, J, D], BF16, name="xr%d" % g) for g in range(NG)]
         gr = [None] * NG
         pt = [None] * NT
         rb = [None] * NT
+        kraw = [None] * NCHUNK
 
         def load_x(g, j0, j1):
             nc.sync.dma_start(out=xr[g][:, j0:j1, :], in_=x_v[:, g, j0:j1, :])
@@ -134,61 +125,42 @@ def tile_rbf_softmax_layer_t_v_kernel(tc, x, kernel, rbf, probs, grad_out, out_0
             rb[r] = rpool.tile([P, C], F32, name="rb", tag="rb")
             nc.sync.dma_start(out=rb[r][:], in_=rb_v[:, r // J, r % J, :])
 
-        dma_plan = [
-            ("k", 0), ("k", 1), ("k", 2), ("k", 3), ("x", 0, 0, 2), ("r", 0), ("p", 0), ("g", 0, 0, 2), ("r", 1), ("p", 1),
-            ("r", 2), ("p", 2), ("x", 0, 2, 4), ("g", 0, 2, 4), ("r", 3), ("p", 3), ("x", 1, 0, 4), ("r", 4), ("p", 4),
-            ("g", 1, 0, 4), ("r", 5), ("p", 5), ("x", 2, 0, 4),
-        ]
-        kraw = [None] * 4
+        def load_tile(r):
+            load_r(r)
+            load_p(r)
+
         alloc_g(0)
         alloc_g(1)
-        for item in dma_plan:
-            if item[0] == "x":
-                load_x(item[1], item[2], item[3])
-            if item[0] == "g":
-                load_g(item[1], item[2], item[3])
-            if item[0] == "r":
-                load_r(item[1])
-            if item[0] == "p":
-                load_p(item[1])
-            if item[0] == "k":
-                c = item[1]
-                kraw[c] = st.tile([P, 2, C], BF16, name="kraw%d" % c, tag="st")
-                nc.sync.dma_start(out=kraw[c][:], in_=k_v[:, 2 * c : 2 * c + 2, :])
+        for ch in range(NCHUNK):
+            kraw[ch] = st.tile([P, 2, C], BF16, name="kraw%d" % ch, tag="st")
+            nc.sync.dma_start(out=kraw[ch][:], in_=k_v[:, 2 * ch : 2 * ch + 2, :])
+        load_x(0, 0, 2)
+        load_tile(0)
+        load_g(0, 0, 2)
+        load_tile(1)
+        load_tile(2)
+        load_x(0, 2, 4)
+        load_g(0, 2, 4)
+        load_tile(3)
+        load_x(1, 0, 4)
+        load_tile(4)
+        load_g(1, 0, 4)
+        load_tile(5)
+        load_x(2, 0, 4)
+
+        def loads_after(r):
+            if r + RING < NT:
+                load_p(r + RING)
+                load_r(r + RING)
 
         def rx_sq(r):
             nc.scalar.activation(out=junk_s[:], in_=xr[r // J][:, r % J, :], func=ACT.Square, accum_out=ssx[:, r : r + 1])
 
-        def rx_fin_v(c0, c1):
+        def rx_fin(c0, c1):
             nc.vector.tensor_scalar(out=tx[:, c0:c1], in0=ssx[:, c0:c1], scalar1=EPS, scalar2=None, op0=ALU.max, op1=ALU.add, accum_out=tjunk[:, 0:1])
             nc.vector.reciprocal(out=rx2[:, c0:c1], in_=tx[:, c0:c1])
-
-        def rx_fin_s(c0, c1):
             nc.scalar.activation(out=rx[:, c0:c1], in_=rx2[:, c0:c1], func=ACT.Sqrt)
             nc.scalar.activation(out=nrx2[:, c0:c1], in_=rx2[:, c0:c1], func=ACT.Copy, scale=-1.0)
-
-        def s_scale(r):
-            nc.scalar.activation(out=rb[r][:], in_=rb[r][:], func=ACT.Copy, scale=rx[:, r : r + 1])
-
-        def g_mul1(r):
-            for n in range(GSPLIT):
-                cs = slice(C // GSPLIT * n, C // GSPLIT * (n + 1))
-                nc.gpsimd.tensor_tensor(out=rb[r][:, cs], in0=rb[r][:, cs], in1=pt[r][:, cs], op=ALU.mult)
-
-        def g_mul2(r):
-            for n in range(GSPLIT):
-                cs = slice(C // GSPLIT * n, C // GSPLIT * (n + 1))
-                nc.gpsimd.tensor_tensor(out=rb[r][:, cs], in0=rb[r][:, cs], in1=rkb[:, cs], op=ALU.mult)
-
-        def g_mul(r):
-            g_mul1(r)
-            g_mul2(r)
-
-        def v_mul1(r):
-            nc.vector.scalar_tensor_tensor(out=rb[r][:], in0=pt[r][:], scalar=rx[:, r : r + 1], in1=rb[r][:], op0=ALU.mult, op1=ALU.mult)
-
-        def v_mul2(r):
-            nc.vector.tensor_tensor(out=rb[r][:], in0=rb[r][:], in1=rkb[:], op=ALU.mult)
 
         gps = [None] * NT
         rp = []
@@ -200,194 +172,191 @@ def tile_rbf_softmax_layer_t_v_kernel(tc, x, kernel, rbf, probs, grad_out, out_0
         tsc = [None] * NPAIR
         aps = [None] * NT
         dx = [None] * NT
+        tps = {}
 
-        def warm(n, b, d):
-            if n > 0:
-                wps = bank(b, [P, H], F32, "wps")
-                for k in range(n):
-                    nc.tensor.matmul_mx(out=wps[:], lhsT=tcd[d][:, 0:P].bitcast(E5), lhsT_scale=tsc[d][:, 0:P], rhs=ktc[:, 0, 0:H].bitcast(E4), rhs_scale=kts[:, 0, 0:H], start=True, stop=True)
+        def g_mul1(r):
+            nc.gpsimd.tensor_tensor(out=rb[r][:, 0:C], in0=rb[r][:, 0:C], in1=pt[r][:, 0:C], op=ALU.mult)
+
+        def g_mul2(r):
+            nc.gpsimd.tensor_tensor(out=rb[r][:, 0:C], in0=rb[r][:, 0:C], in1=rkb[:, 0:C], op=ALU.mult)
+
+        def g_mul(r):
+            g_mul1(r)
+            g_mul2(r)
+
+        def s_scale(r):
+            nc.scalar.activation(out=rb[r][:], in_=rb[r][:], func=ACT.Copy, scale=rx[:, r : r + 1])
+
+        def v_mul(r):
+            nc.vector.scalar_tensor_tensor(out=rb[r][:], in0=pt[r][:], scalar=rx[:, r : r + 1], in1=rb[r][:], op0=ALU.mult, op1=ALU.mult)
 
         def gcopy(r):
             gps[r] = bank(r % 2, [P, C], BF16, "gps")
-            for n in range(2):
+            for n in range(NH):
                 nc.tensor.matmul(out=gps[r][:, H * n : H * n + H], lhsT=ident_b[:], rhs=gr[r // J][:, r % J, H * n : H * n + H], start=True, stop=True)
 
-        def op_a(r):
+        def row_sum(r):
             nc.vector.scalar_tensor_tensor(out=junk_v[:], in0=gps[r][:], scalar=1.0, in1=pt[r][:], op0=ALU.mult, op1=ALU.mult, accum_out=s_all[:, r : r + 1])
 
-        def op_f(r):
-            g = r // J
+        def alloc_dz(r):
             if r % J == 0:
-                dz[g] = dzpool.tile([P, J, C], BF16, name="dz", tag="dz")
-            nc.vector.scalar_tensor_tensor(out=dz[g][:, r % J, :], in0=gps[r][:], scalar=s_all[:, r : r + 1], in1=rb[r][:], op0=ALU.subtract, op1=ALU.mult)
+                dz[r // J] = dzpool.tile([P, J, C], BF16, name="dz", tag="dz")
 
-        def op_w(r):
+        def make_dz(r):
+            alloc_dz(r)
+            nc.vector.scalar_tensor_tensor(out=dz[r // J][:, r % J, :], in0=gps[r][:], scalar=s_all[:, r : r + 1], in1=rb[r][:], op0=ALU.subtract, op1=ALU.mult)
+
+        def make_dz_without_rk(r):
             nc.vector.scalar_tensor_tensor(out=rb[r][:], in0=gps[r][:], scalar=s_all[:, r : r + 1], in1=rb[r][:], op0=ALU.subtract, op1=ALU.mult)
 
-        def op_f2(r):
-            g = r // J
-            if r % J == 0:
-                dz[g] = dzpool.tile([P, J, C], BF16, name="dz", tag="dz")
-            for n in range(2):
-                nc.vector.tensor_tensor(out=dz[g][:, r % J, H * n : H * n + H], in0=rb[r][:, H * n : H * n + H], in1=rp[n][:], op=ALU.mult)
+        def times_rk(r):
+            alloc_dz(r)
+            for n in range(NH):
+                nc.vector.tensor_tensor(out=dz[r // J][:, r % J, H * n : H * n + H], in0=rb[r][:, H * n : H * n + H], in1=rp[n][:], op=ALU.mult)
 
         def alloc_tgp(d):
-            tgp[d] = tgpool.tile([P, 2, 2, P, 4], BF16, name="tgp", tag="tgp", align_bytes=64)
+            tgp[d] = tgpool.tile([P, 2, NH, P, J], BF16, name="tgp", tag="tgp", align_bytes=64)
 
-        tpss = {}
-
-        def op_t(r):
-            tps = bank(2 + r % 2, [P, 2, 2, P], F32, "tps")
-            tpss[r] = tps
+        def transpose_dz(r):
+            tps[r] = bank(2 + r % 2, [P, NH, 2, P], F32, "tps")
             w = dz[r // J][:, r % J, :].bitcast(F32)
-            for h in range(2):
+            for h in range(NH):
                 for u in range(2):
-                    nc.tensor.transpose(tps[:, h, u, :], w[:, 256 * h + u : 256 * (h + 1) : 2], ident_f[:])
+                    nc.tensor.transpose(tps[r][:, h, u, :], w[:, WORDS * h + u : WORDS * (h + 1) : 2], ident_f[:])
 
-        def op_c(r):
-            d = r // 2
-            tps = tpss[r]
-            dst = tgp[d][:, r % 2].rearrange("q h p t -> q (h p t)").bitcast(F32).rearrange("q (h p u) -> q h p u", h=2, u=2)
-            nc.scalar.copy(out=dst, in_=tps[:].rearrange("q h u p -> q h p u"))
+        def copy_dz_t(r):
+            dst = tgp[r // 2][:, r % 2].rearrange("q h p t -> q (h p t)").bitcast(F32).rearrange("q (h p u) -> q h p u", h=NH, u=2)
+            nc.scalar.copy(out=dst, in_=tps[r][:].rearrange("q h u p -> q h p u"))
 
-        def op_q(d):
-            tcd[d] = tcpool.tile([P, 4 * P], U32, name="tcd", tag="tcd", align_bytes=64)
-            tsc[d] = tcpool.tile([P, 4 * P], U8, name="tsc", tag="tsc", align_bytes=64)
+        def quantize_pair(d):
+            tcd[d] = tcpool.tile([P, 2 * NH * P], U32, name="tcd", tag="tcd", align_bytes=64)
+            tsc[d] = tcpool.tile([P, 2 * NH * P], U8, name="tsc", tag="tsc", align_bytes=64)
             nc.vector.quantize_mx(out=tcd[d][:].bitcast(E5), scales=tsc[d][:], in_=tgp[d][:].rearrange("q i h p t -> q (i h p t)"))
-            if RENDEZVOUS:
-                alloc_tgp(d + 2)
-                nc.gpsimd.memset(tgp[d + 2][:, 0, 0, 0:4, :], 0.0)
-            elif d + 2 < NPAIR:
-                alloc_tgp(d + 2)
+            alloc_tgp(d + 2)
+            nc.gpsimd.memset(tgp[d + 2][:, 0, 0, 0:4, :], 0.0)
 
-        def op_mm(r, b0=None):
-            d = r // 2
-            if b0 is None:
-                b0 = 4 + 2 * (r % 2)
+        def product_a(r, b0):
             aps[r] = [bank(b0, [P, H], F32, "aps"), bank(b0 + 1, [P, H], F32, "aps")]
-            for n in range(2):
-                for h in range(2):
-                    c0 = P * (2 * (r % 2) + h)
+            for n in range(NH):
+                for h in range(NH):
+                    c0 = P * (NH * (r % 2) + h)
                     nc.tensor.matmul_mx(
                         out=aps[r][n][:],
-                        lhsT=tcd[d][:, c0 : c0 + P].bitcast(E5),
-                        lhsT_scale=tsc[d][:, c0 : c0 + P],
+                        lhsT=tcd[r // 2][:, c0 : c0 + P].bitcast(E5),
+                        lhsT_scale=tsc[r // 2][:, c0 : c0 + P],
                         rhs=ktc[:, h, H * n : H * n + H].bitcast(E4),
                         rhs_scale=kts[:, h, H * n : H * n + H],
                         start=(h == 0),
-                        stop=(h == 1),
+                        stop=(h == NH - 1),
                     )
 
-        def op_e0a(r):
-            for n in range(2):
-                nc.vector.scalar_tensor_tensor(out=junk_v[:, 0:H], in0=aps[r][n][:], scalar=nrx2[:, r : r + 1], in1=xr[r // J][:, r % J, H * n : H * n + H], op0=ALU.mult, op1=ALU.mult, accum_out=sg2[:, 2 * r + n : 2 * r + n + 1])
-            if r >= 11:
-                return
+        def x_row(r):
+            return xr[r // J][:, r % J, :]
+
+        def project_sum(r):
+            for n in range(NH):
+                nc.vector.scalar_tensor_tensor(out=junk_v[:, 0:H], in0=aps[r][n][:], scalar=nrx2[:, r : r + 1], in1=x_row(r)[:, H * n : H * n + H], op0=ALU.mult, op1=ALU.mult, accum_out=sg2[:, 2 * r + n : 2 * r + n + 1])
             nc.scalar.activation(out=sg[:, r : r + 1], in_=sg2[:, 2 * r : 2 * r + 1], func=ACT.Identity, bias=sg2[:, 2 * r + 1 : 2 * r + 2])
 
-        def loads_after(r):
-            if r + 6 < NT:
-                load_p(r + 6)
-                load_r(r + 6)
-
-        def op_e0b(r):
+        def project(r):
             dx[r] = st.tile([P, D], F32, name="dx", tag="st")
-            for n in range(2):
-                nc.vector.scalar_tensor_tensor(out=dx[r][:, H * n : H * n + H], in0=xr[r // J][:, r % J, H * n : H * n + H], scalar=(sg[:, r : r + 1] if r < 10 else sgv[:, r - 10 : r - 9]), in1=aps[r][n][:], op0=ALU.mult, op1=ALU.add)
-                if r == NT - 1:
-                    nc.sync.dma_start(out=o0_v[:, r // J, r % J, H * n : H * n + H], in_=dx[r][:, H * n : H * n + H])
-            if r < NT - 1:
-                nc.sync.dma_start(out=o0_v[:, r // J, r % J, :], in_=dx[r][:])
+            for n in range(NH):
+                nc.vector.scalar_tensor_tensor(out=dx[r][:, H * n : H * n + H], in0=x_row(r)[:, H * n : H * n + H], scalar=sg[:, r : r + 1], in1=aps[r][n][:], op0=ALU.mult, op1=ALU.add)
+            nc.sync.dma_start(out=o0_v[:, r // J, r % J, :], in_=dx[r][:])
 
-        def dzil(g, q):
-            if q == 0:
+        asb = {}
+        prod = {}
+
+        def far_copy(r):
+            asb[r] = ppool.tile([P, D], F32, name="gpa", tag="pt")
+            for n in range(NH):
+                nc.scalar.copy(out=asb[r][:, H * n : H * n + H], in_=aps[r][n][:])
+
+        def far_product(r):
+            prod[r] = rpool.tile([P, D], F32, name="gpp", tag="rb")
+            nc.gpsimd.tensor_tensor(out=prod[r][:], in0=asb[r][:], in1=x_row(r), op=ALU.mult)
+
+        def far_sum(r):
+            nc.scalar.activation(out=junk_s[:], in_=prod[r][:], func=ACT.Copy, scale=nrx2[:, r : r + 1], accum_out=sgs[:, r : r + 1])
+
+        def far_project(r):
+            dx[r] = st.tile([P, D], F32, name="dx", tag="st")
+            nc.gpsimd.tensor_scalar(out=prod[r][:], in0=x_row(r), scalar1=sgs[:, r : r + 1], scalar2=0.0, op0=ALU.mult, op1=ALU.add)
+            nc.gpsimd.tensor_tensor(out=dx[r][:], in0=prod[r][:], in1=asb[r][:], op=ALU.add)
+            nc.sync.dma_start(out=o0_v[:, r // J, r % J, :], in_=dx[r][:])
+
+        def interleave_dz(g, piece, eng):
+            if piece == 0:
                 dzg[g] = ilv.tile([P, C, J], BF16, name="dzg", tag="ilv", align_bytes=64)
-            ws = slice(256 * q, 256 * q + 256)
-            nc.scalar.copy(out=dzg[g][:, ws, :], in_=dz[g][:, :, ws].rearrange("p j w -> p w j"))
+            ws = slice(PIECE * piece, PIECE * piece + PIECE)
+            if eng == "G":
+                nc.gpsimd.tensor_scalar(out=dzg[g][:, ws, :], in0=dz[g][:, :, ws].rearrange("p j w -> p w j"), scalar1=1.0, scalar2=0.0, op0=ALU.mult, op1=ALU.add)
+            else:
+                nc.scalar.copy(out=dzg[g][:, ws, :], in_=dz[g][:, :, ws].rearrange("p j w -> p w j"))
 
-        def dzil_g(g, q):
-            ws = slice(256 * q, 256 * q + 256)
-            nc.gpsimd.tensor_scalar(out=dzg[g][:, ws, :], in0=dz[g][:, :, ws].rearrange("p j w -> p w j"), scalar1=1.0, scalar2=0.0, op0=ALU.mult, op1=ALU.add)
-
-        def qd(g):
+        def quantize_dz(g):
             nc.vector.quantize_mx(out=dzc[:, g, :].bitcast(E5), scales=dzs[:, g, :], in_=dzg[g][:].rearrange("p w j -> p (w j)"))
 
-        def xil(g, q, eng):
-            if q == 0:
+        def interleave_x(g, piece, eng):
+            if piece == 0:
                 xg[g] = ilv.tile([P, D, J], BF16, name="xg", tag="ilv", align_bytes=64)
-            ws = slice(256 * q, 256 * q + 256)
+            ws = slice(PIECE * piece, PIECE * piece + PIECE)
             if eng == "G":
                 nc.gpsimd.tensor_scalar(out=xg[g][:, ws, :], in0=xr[g][:, :, ws].rearrange("p j w -> p w j"), scalar1=1.0, scalar2=0.0, op0=ALU.mult, op1=ALU.add)
             else:
                 nc.scalar.copy(out=xg[g][:, ws, :], in_=xr[g][:, :, ws].rearrange("p j w -> p w j"))
 
-        def qx(g):
+        def quantize_x(g):
             nc.vector.quantize_mx(out=xc[:, g, :].bitcast(E4), scales=xs[:, g, :], in_=xg[g][:].rearrange("p w j -> p (w j)"))
 
         ring = [6, 7, 4, 5]
         ring_at = [0]
+        ktg = [None] * NH
+        tb = {}
+        kb = {}
 
         def next_bank():
             b = ring[ring_at[0] % 4]
             ring_at[0] = ring_at[0] + 1
             return b
 
-        ktg = [None] * 2
-
-        tbs = {}
-
-        def ktg_t(h, c):
-            tb = bank(next_bank(), [P, 2, 2, P], F32, "tb")
-            tbs[(h, c)] = tb
+        def transpose_k_words(h, ch):
+            tb[(h, ch)] = bank(next_bank(), [P, 2, 2, P], F32, "tb")
             for a2 in range(2):
-                kw = kraw[c][:, a2, :].bitcast(F32)
+                kw = kraw[ch][:, a2, :].bitcast(F32)
                 for u in range(2):
-                    nc.tensor.transpose(tb[:, a2, u, :], kw[:, 256 * h + u : 256 * (h + 1) : 2], ident_f[:])
+                    nc.tensor.transpose(tb[(h, ch)][:, a2, u, :], kw[:, WORDS * h + u : WORDS * (h + 1) : 2], ident_f[:])
 
-        def ktg_c(h, c, eng):
-            if c == 0:
-                ktg[h] = ilv.tile([P, D, 4], BF16, name="ktg", tag="ilv", align_bytes=64)
+        def copy_k_words(h, ch, eng):
+            if ch == 0:
+                ktg[h] = ilv.tile([P, D, J], BF16, name="ktg", tag="ilv", align_bytes=64)
             ktw = ktg[h][:].rearrange("q f t -> q (f t)").bitcast(F32)
-            tb = tbs[(h, c)]
-            dst = ktw[:, 512 * c : 512 * c + 512].rearrange("q (a f u) -> q a f u", a=2, u=2)
+            dst = ktw[:, H * ch : H * ch + H].rearrange("q (a f u) -> q a f u", a=2, u=2)
             if eng == "V":
-                nc.vector.tensor_copy(out=dst, in_=tb[:].rearrange("q a u f -> q a f u"))
+                nc.vector.tensor_copy(out=dst, in_=tb[(h, ch)][:].rearrange("q a u f -> q a f u"))
             else:
-                nc.scalar.copy(out=dst, in_=tb[:].rearrange("q a u f -> q a f u"))
+                nc.scalar.copy(out=dst, in_=tb[(h, ch)][:].rearrange("q a u f -> q a f u"))
 
-        def s_item(it):
-            if it[0] == "rx":
-                rx_sq(it[1])
-            if it[0] == "xil":
-                xil(it[1], it[2], "S")
-            if it[0] == "dzil":
-                dzil(it[1], it[2])
-
-        def ktg_q(h):
+        def quantize_k(h):
             nc.vector.quantize_mx(out=ktc[:, h, :].bitcast(E4), scales=kts[:, h, :], in_=ktg[h][:].rearrange("q f t -> q (f t)"))
 
-        kbs = {}
+        def transpose_k_block(m):
+            kb[m] = bank(next_bank(), [P, D], BF16, "kb")
+            for a in range(NB):
+                nc.tensor.transpose(kb[m][:, a * P : (a + 1) * P], kraw[a // 2][:, a % 2, m * P : (m + 1) * P], ident_b[:])
 
-        def ktn_t(m):
-            kbs[m] = bank(next_bank(), [P, D], BF16, "kb")
-            for a in range(8):
-                nc.tensor.transpose(kbs[m][:, a * P : (a + 1) * P], kraw[a // 2][:, a % 2, m * P : (m + 1) * P], ident_b[:])
+        def copy_k_block(m):
+            nc.scalar.copy(out=ktn[:, m, :], in_=kb[m][:])
 
-        def ktn_c(m, eng):
-            kbm = kbs[m]
-            if eng == "V":
-                nc.vector.tensor_copy(out=ktn[:, m, :], in_=kbm[:])
-            else:
-                nc.scalar.copy(out=ktn[:, m, :], in_=kbm[:])
+        cps = [None] * NB
+        dk = [None] * NB
+        o1 = {}
 
-        cps = [None] * 8
-        dk = [None] * 8
-
-        def c_alloc(m, b):
+        def alloc_c(m, b):
             cps[m] = [bank(b[0], [P, H], F32, "cps"), bank(b[1], [P, H], F32, "cps")]
 
-        def c_mm(m, gs):
-            for n in range(2):
+        def product_c(m, gs):
+            for n in range(NH):
                 for g in gs:
                     nc.tensor.matmul_mx(
                         out=cps[m][n][:],
@@ -399,299 +368,222 @@ def tile_rbf_softmax_layer_t_v_kernel(tc, x, kernel, rbf, probs, grad_out, out_0
                         stop=(g == NG - 1),
                     )
 
-        def e1a(m, n):
-            nc.vector.scalar_tensor_tensor(out=junk_v[:, 0:H], in0=cps[m][n][:], scalar=nrk2[:, cm(m) : cm(m) + 1], in1=ktn[:, m, H * n : H * n + H], op0=ALU.mult, op1=ALU.mult, accum_out=cg2[:, 2 * m + n : 2 * m + n + 1])
+        def c_sum(m, n):
+            nc.vector.scalar_tensor_tensor(out=junk_v[:, 0:H], in0=cps[m][n][:], scalar=nrk2[:, kcol(m) : kcol(m) + 1], in1=ktn[:, m, H * n : H * n + H], op0=ALU.mult, op1=ALU.mult, accum_out=cg2[:, 2 * m + n : 2 * m + n + 1])
 
-        def e1s(m):
+        def c_total(m):
             nc.vector.tensor_tensor(out=cg[:, m : m + 1], in0=cg2[:, 2 * m : 2 * m + 1], in1=cg2[:, 2 * m + 1 : 2 * m + 2], op=ALU.add)
 
-        def e1b(m, n):
+        def c_project(m, n):
             if n == 0:
                 dk[m] = st.tile([P, D], F32, name="dk", tag="st")
             nc.vector.scalar_tensor_tensor(out=dk[m][:, H * n : H * n + H], in0=ktn[:, m, H * n : H * n + H], scalar=cg[:, m : m + 1], in1=cps[m][n][:], op0=ALU.mult, op1=ALU.add)
 
-        o1 = {}
-
-        def e1c(m, hfs):
-            if hfs[0] == 0:
-                o1[m] = rpool.tile([P, 8, P], F32, name="o1s", tag="rb")
-            o1s = o1[m]
-            for hf in hfs:
-                bt = bank((6 if m < 6 else (4 if m == 6 else 0)) + hf, [P, 4, P], F32, "bt")
+        def c_store(m):
+            o1[m] = rpool.tile([P, NB, P], F32, name="o1s", tag="rb")
+            b0 = 6 if m < 6 else (4 if m == 6 else 0)
+            for hf in range(2):
+                bt = bank(b0 + hf, [P, 4, P], F32, "bt")
                 for a in range(4):
                     nc.tensor.transpose(bt[:, a, :], dk[m][:, P * (4 * hf + a) : P * (4 * hf + a) + P], ident_f[:])
-                if m == 7:
-                    nc.vector.tensor_copy(out=o1s[:, 4 * hf : 4 * hf + 4, :], in_=bt[:])
-                    nc.sync.dma_start(out=o1_v[:, 4 * hf : 4 * hf + 4, P * m : P * m + P], in_=o1s[:, 4 * hf : 4 * hf + 4, :])
+                if m == NB - 1:
+                    nc.vector.tensor_copy(out=o1[m][:, 4 * hf : 4 * hf + 4, :], in_=bt[:])
+                    nc.sync.dma_start(out=o1_v[:, 4 * hf : 4 * hf + 4, P * m : P * m + P], in_=o1[m][:, 4 * hf : 4 * hf + 4, :])
                 else:
-                    nc.scalar.copy(out=o1s[:, 4 * hf : 4 * hf + 4, :], in_=bt[:])
-            if m < 7:
-                nc.scalar.dma_start(out=o1_v[:, :, P * m : P * m + P], in_=o1s[:])
-
-
-        sgs = keep.tile([P, 16], F32, name="sgs")
-        sgv = keep.tile([P, 8], F32, name="sgv")
-        gp_a = {}
-        gp_p = {}
-
-        def gp_copy(key, ps):
-            gp_a[key] = ppool.tile([P, D], F32, name="gpa", tag="pt")
-            for n in range(2):
-                nc.scalar.copy(out=gp_a[key][:, H * n : H * n + H], in_=ps[n][:])
-
-        def gp_prod(key, opnd):
-            gp_p[key] = rpool.tile([P, D], F32, name="gpp", tag="rb")
-            nc.gpsimd.tensor_tensor(out=gp_p[key][:], in0=gp_a[key][:], in1=opnd, op=ALU.mult)
-
-        def gp_sum(key, col, nr2):
-            nc.scalar.activation(out=junk_s[:], in_=gp_p[key][:], func=ACT.Copy, scale=nr2, accum_out=sgs[:, col : col + 1])
-
-        def gp_fin(key, col, opnd, out):
-            nc.gpsimd.tensor_scalar(out=gp_p[key][:], in0=opnd, scalar1=sgs[:, col : col + 1], scalar2=0.0, op0=ALU.mult, op1=ALU.add)
-            nc.gpsimd.tensor_tensor(out=out, in0=gp_p[key][:], in1=gp_a[key][:], op=ALU.add)
-
-        def x_row(r):
-            return xr[r // J][:, r % J, :]
+                    nc.scalar.copy(out=o1[m][:, 4 * hf : 4 * hf + 4, :], in_=bt[:])
+            if m < NB - 1:
+                nc.scalar.dma_start(out=o1_v[:, :, P * m : P * m + P], in_=o1[m][:])
 
         gb = [bank(m, [P, P], F32, "gb") for m in range(NGRAM)]
-        kb = [None] * 8
-        for m in range(NGRAM, 8):
+        for m in range(NGRAM, NB):
             kb[m] = bank(m, [P, D], BF16, "kb")
-        for a in range(8):
+        for a in range(NB):
             ka = kraw[a // 2][:, a % 2, :]
             for m in range(NGRAM):
-                nc.tensor.matmul(out=gb[m][:], lhsT=ka[:, m * P : (m + 1) * P], rhs=ka[:, m * P : (m + 1) * P], start=(a == 0), stop=(a == 7))
-            for m in range(NGRAM, 8):
+                nc.tensor.matmul(out=gb[m][:], lhsT=ka[:, m * P : (m + 1) * P], rhs=ka[:, m * P : (m + 1) * P], start=(a == 0), stop=(a == NB - 1))
+            for m in range(NGRAM, NB):
                 nc.tensor.transpose(kb[m][:, a * P : (a + 1) * P], ka[:, m * P : (m + 1) * P], ident_b[:])
         rx_sq(0)
         rx_sq(1)
-        nc.scalar.activation(out=junk_s[:], in_=kb[6][:], func=ACT.Square, accum_out=ssk[:, cm(6) : cm(6) + 1])
+        nc.scalar.activation(out=junk_s[:], in_=kb[6][:], func=ACT.Square, accum_out=ssk[:, kcol(6) : kcol(6) + 1])
         for m in range(NGRAM):
             nc.vector.scalar_tensor_tensor(out=junk_v[:, 0:P], in0=gb[m][:], scalar=1.0, in1=ident_f[:], op0=ALU.mult, op1=ALU.mult, accum_out=ssk[:, m : m + 1])
-        rx_fin_v(0, 2)
-        rx_fin_s(0, 2)
-        nc.scalar.activation(out=junk_s[:], in_=kb[7][:], func=ACT.Square, accum_out=ssk[:, cm(7) : cm(7) + 1])
+        rx_fin(0, 2)
+        nc.scalar.activation(out=junk_s[:], in_=kb[7][:], func=ACT.Square, accum_out=ssk[:, kcol(7) : kcol(7) + 1])
         gcopy(0)
         gcopy(1)
-        v_mul1(0)
-        for m in range(NGRAM, 8):
-            nc.scalar.copy(out=ktn[:, m, :], in_=kb[m][:])
-        op_a(0)
+        v_mul(0)
+        for m in range(NGRAM, NB):
+            copy_k_block(m)
+        row_sum(0)
         nc.vector.tensor_scalar(out=tk[:], in0=ssk[:], scalar1=EPS, scalar2=None, op0=ALU.max, op1=ALU.add, accum_out=tjunk[:, 1:2])
         nc.vector.reciprocal(out=rk2[:], in_=tk[:])
         nc.scalar.activation(out=rk10[:], in_=rk2[:], func=ACT.Sqrt, scale=100.0)
         nc.scalar.activation(out=nrk2[:], in_=rk2[:], func=ACT.Copy, scale=-1.0)
-        ktg_t(0, 0)
-        ktg_t(0, 1)
+        transpose_k_words(0, 0)
+        transpose_k_words(0, 1)
         rp.append(bank(4, [P, H], F32, "rp"))
         rp.append(bank(5, [P, H], F32, "rp"))
-        for m in range(8):
-            nc.tensor.transpose(rp[m // 4][:, (m % 4) * P : (m % 4 + 1) * P], rk10[:, cm(m) : cm(m) + 1].to_broadcast([P, P]), ident_f[:])
-        v_mul1(1)
-        op_w(0)
+        for m in range(NB):
+            nc.tensor.transpose(rp[m // 4][:, (m % 4) * P : (m % 4 + 1) * P], rk10[:, kcol(m) : kcol(m) + 1].to_broadcast([P, P]), ident_f[:])
+        v_mul(1)
+        make_dz_without_rk(0)
         nc.scalar.copy(out=rkb[:, 0:H], in_=rp[0][:])
         nc.scalar.copy(out=rkb[:, H:C], in_=rp[1][:])
-        op_a(1)
+        row_sum(1)
         g_mul(2)
         alloc_tgp(0)
         alloc_tgp(1)
         gcopy(2)
-        op_f2(0)
+        times_rk(0)
         loads_after(0)
-        op_t(0)
+        transpose_dz(0)
         rx_sq(2)
         rx_sq(3)
-        op_w(1)
+        make_dz_without_rk(1)
         gcopy(3)
-        op_f2(1)
+        times_rk(1)
         loads_after(1)
-        op_t(1)
-        op_c(0)
-        rx_fin_v(2, 4)
-        rx_fin_s(2, 4)
+        transpose_dz(1)
+        copy_dz_t(0)
+        rx_fin(2, 4)
         g_mul(3)
         s_scale(2)
-        ktg_t(0, 2)
-        ktg_t(0, 3)
-        op_a(2)
-        op_a(3)
+        transpose_k_words(0, 2)
+        transpose_k_words(0, 3)
+        row_sum(2)
+        row_sum(3)
         rx_sq(4)
-        op_c(1)
+        copy_dz_t(1)
         rx_sq(5)
         rx_sq(6)
-        op_f(2)
+        make_dz(2)
         loads_after(2)
-        op_t(2)
+        transpose_dz(2)
         g_mul(4)
-        for c in range(4):
-            ktg_c(0, c, "V")
-            ktg_t(1, c)
+        for ch in range(NCHUNK):
+            copy_k_words(0, ch, "V")
+            transpose_k_words(1, ch)
         s_scale(3)
-        op_c(2)
+        copy_dz_t(2)
         rx_sq(7)
-        ktg_q(0)
-        op_f(3)
+        quantize_k(0)
+        make_dz(3)
         loads_after(3)
         alloc_g(2)
         load_g(2, 0, 4)
         gcopy(4)
-        op_t(3)
+        transpose_dz(3)
         gcopy(5)
-        for c in range(3):
-            ktg_c(1, c, "S")
-            ktn_t(c)
-        op_c(3)
-        ktg_c(1, 3, "S")
-        ktn_t(3)
-        op_q(0)
+        for ch in range(3):
+            copy_k_words(1, ch, "S")
+            transpose_k_block(ch)
+        copy_dz_t(3)
+        copy_k_words(1, 3, "S")
+        transpose_k_block(3)
+        quantize_pair(0)
         g_mul(5)
-        rx_fin_v(4, 8)
-        rx_fin_s(4, 8)
-        op_a(4)
-        op_a(5)
+        rx_fin(4, 8)
+        row_sum(4)
+        row_sum(5)
         for m in range(4):
-            ktn_c(m, "S")
+            copy_k_block(m)
             if m + 4 < NGRAM:
-                ktn_t(m + 4)
+                transpose_k_block(m + 4)
         for m in range(4, NGRAM):
-            ktn_c(m, "S")
-        ktg_q(1)
-        op_q(1)
-        op_mm(0)
-        op_mm(1)
-        for r in range(6, 6 + 2 * (GLEAD - 1)):
-            g_mul(r)
+            copy_k_block(m)
+        quantize_k(1)
+        quantize_pair(1)
+        product_a(0, 4)
+        product_a(1, 6)
+        g_mul(6)
+        g_mul(7)
 
         for d in range(2, NPAIR):
-            e = d - 2
-            op_e0a(2 * e)
-            op_e0a(2 * e + 1)
+            lo, hi = 2 * d, 2 * d + 1
+            project_sum(lo - 4)
+            project_sum(hi - 4)
             if d == 4:
-                rx_fin_v(8, 12)
-                rx_fin_s(8, 12)
-            if d in (3, 5):
-                qd(d // 2 - 1)
-            if d == 6:
-                qx(0)
-            if 3 <= d <= NPAIR:
-                op_q(d - 1)
-            op_e0b(2 * e)
-            op_e0b(2 * e + 1)
-            if d < NPAIR:
-                op_mm(2 * d - 2)
-                op_mm(2 * d - 1)
-                warm(W_MID, 2, d - 1)
-            for r in (2 * d + 2 * GLEAD, 2 * d + 2 * GLEAD + 1):
-                if r < NT:
-                    g_mul(r)
-            if d in (4, 5):
-                for q in range(4):
-                    xil(d - 4, q, "G")
-            if d in (2, 4, 6):
-                dzil(d // 2 - 1, 0)
-            if d < NPAIR:
-                s_scale(2 * d)
-                s_scale(2 * d + 1)
-            if d in (2, 4, 6):
-                for q in range(1, 4):
-                    dzil(d // 2 - 1, q)
+                rx_fin(8, 12)
+            if d % 2 == 1:
+                quantize_dz(d // 2 - 1)
+            if d > 2:
+                quantize_pair(d - 1)
+            project(lo - 4)
+            project(hi - 4)
+            product_a(lo - 2, 4)
+            product_a(hi - 2, 6)
+            if hi + 4 < NT:
+                g_mul(lo + 4)
+                g_mul(hi + 4)
+            else:
+                for piece in range(4):
+                    interleave_x(d - 4, piece, "G")
+            if d % 2 == 0:
+                interleave_dz(d // 2 - 1, 0, "S")
+            s_scale(lo)
+            s_scale(hi)
+            if d % 2 == 0:
+                for piece in range(1, 4):
+                    interleave_dz(d // 2 - 1, piece, "S")
             if d == 3:
                 for r in range(8, 12):
                     rx_sq(r)
             if d == 5:
-                for q in range(4):
-                    xil(2, q, "S")
-            if d < NPAIR:
-                if d > 2:
-                    op_a(2 * d)
-                    op_a(2 * d + 1)
-                for r in (2 * d, 2 * d + 1):
-                    op_f(r)
-                    loads_after(r)
-                    op_t(r)
-                    op_c(r)
-                if d + 1 < NPAIR:
-                    gcopy(2 * d + 2)
-                    gcopy(2 * d + 3)
-                warm(W_END, 2, d - 1)
-                warm(W_END, 3, d - 1)
+                for piece in range(4):
+                    interleave_x(2, piece, "S")
+            if d > 2:
+                row_sum(lo)
+                row_sum(hi)
+            for r in (lo, hi):
+                make_dz(r)
+                loads_after(r)
+                transpose_dz(r)
+                copy_dz_t(r)
+            if d + 1 < NPAIR:
+                gcopy(lo + 2)
+                gcopy(hi + 2)
 
-        def k_row(m):
-            return ktn[:, m, :]
-
-        def gx_fin(t):
-            dx[t] = st.tile([P, D], F32, name="dx", tag="st")
-            gp_fin(("x", t), t, x_row(t), dx[t][:])
-            nc.sync.dma_start(out=o0_v[:, t // J, t % J, :], in_=dx[t][:])
-
-        def gk_fin(m):
-            dk[m] = st.tile([P, D], F32, name="dk", tag="st")
-            gp_fin(("k", m), 12 + m, k_row(m), dk[m][:])
-
-        ALLG = (0, 1, 2)
-        vb = [(0, 1), (2, 3), (4, 5)]
-        dzil(2, 0)
-        dzil_g(2, 2)
-        dzil(2, 1)
-        dzil_g(2, 3)
-        op_e0a(8)
-        op_e0a(9)
-        qx(0)
-        op_q(5)
-        op_e0b(8)
-        op_e0b(9)
-        op_mm(10, 4)
-        op_mm(11, 6)
-        qx(1)
-        gp_copy(("x", 10), aps[10])
-        gp_copy(("x", 11), aps[11])
-        gp_prod(("x", 10), x_row(10))
-        gp_prod(("x", 11), x_row(11))
-        c_alloc(0, vb[0])
-        c_mm(0, (0, 1))
-        c_alloc(1, vb[1])
-        c_mm(1, (0, 1))
-        c_alloc(2, vb[2])
-        c_mm(2, (0, 1))
-        qd(2)
-        qx(2)
-        gp_sum(("x", 10), 10, nrx2[:, 10:11])
-        gp_sum(("x", 11), 11, nrx2[:, 11:12])
-        first_v = NGK
-        c_mm(first_v, (2,))
+        pairs_of_banks = [(0, 1), (2, 3), (4, 5)]
+        interleave_dz(2, 0, "S")
+        interleave_dz(2, 2, "G")
+        interleave_dz(2, 1, "S")
+        interleave_dz(2, 3, "G")
+        project_sum(8)
+        project_sum(9)
+        quantize_x(0)
+        quantize_pair(5)
+        project(8)
+        project(9)
+        product_a(10, 4)
+        product_a(11, 6)
+        quantize_x(1)
+        far_copy(10)
+        far_copy(11)
+        far_product(10)
+        far_product(11)
         for m in range(3):
-            if m != first_v:
-                c_mm(m, (2,))
-        for m in range(NGK):
-            gp_copy(("k", m), cps[m])
-            c_alloc(m + 3, vb[m % 3])
-            c_mm(m + 3, ALLG)
-        if NGK > 0:
-            gp_prod(("k", 0), k_row(0))
-        gx_fin(10)
-        gx_fin(11)
-        if NGK > 0:
-            gp_sum(("k", 0), 12, nrk2[:, cm(0) : cm(0) + 1])
-        if NGK > 1:
-            gp_prod(("k", 1), k_row(1))
-            gp_sum(("k", 1), 13, nrk2[:, cm(1) : cm(1) + 1])
-        for m in range(NGK):
-            gk_fin(m)
-        e1a(first_v, 0)
-        e1a(first_v, 1)
-        for m in range(first_v, 8):
-            if m + 1 < 8:
-                e1a(m + 1, 0)
-            e1s(m)
-            if m + 1 < 8:
-                e1a(m + 1, 1)
-            e1b(m, 0)
-            e1b(m, 1)
-            if m + 3 < 8:
-                c_alloc(m + 3, vb[(m + 3) % 3])
-                c_mm(m + 3, ALLG)
-            e1c(m, (0, 1))
-            if m == 4 and NGK > 0:
-                e1c(0, (0, 1))
-            if m == 6 and NGK > 1:
-                e1c(1, (0, 1))
+            alloc_c(m, pairs_of_banks[m])
+            product_c(m, (0, 1))
+        quantize_dz(2)
+        quantize_x(2)
+        far_sum(10)
+        far_sum(11)
+        for m in range(3):
+            product_c(m, (2,))
+        far_project(10)
+        far_project(11)
+        c_sum(0, 0)
+        c_sum(0, 1)
+        for m in range(NB):
+            if m + 1 < NB:
+                c_sum(m + 1, 0)
+            c_total(m)
+            if m + 1 < NB:
+                c_sum(m + 1, 1)
+            c_project(m, 0)
+            c_project(m, 1)
+            if m + 3 < NB:
+                alloc_c(m + 3, pairs_of_banks[m % 3])
+                product_c(m + 3, (0, 1, 2))
+            c_store(m)

from contextlib import ExitStack

import concourse.mybir as mybir
from concourse.masks import make_identity

B, D, C = 1536, 1024, 1024
FLOPS = 2 * 2 * B * D * C

F32 = mybir.dt.float32
BF16 = mybir.dt.bfloat16
U32 = mybir.dt.uint32
U8 = mybir.dt.uint8
E4 = mybir.dt.float8_e4m3fn_x4
E5 = mybir.dt.float8_e5m2_x4
ALU = mybir.AluOpType
ACT = mybir.ActivationFunctionType

P = 128
J = 4
NG = B // (P * J)
NT = NG * J
NPAIR = NT // 2
H = 512
NH = C // H
NB = C // P
PIECE = 256
WORDS = H // 2
RING = 6
NCHUNK = 4
EPS = 1e-12
NGRAM = 6


def tile_rbf_softmax_layer_t_v_kernel(tc, x, kernel, rbf, probs, grad_out, out_0, out_1):
    nc = tc.nc
    x_v = x.rearrange("(g p j) w -> p g j w", p=P, j=J)
    go_v = grad_out.rearrange("(g p j) w -> p g j w", p=P, j=J)
    pr_v = probs.rearrange("(g p j) w -> p g j w", p=P, j=J)
    rb_v = rbf.rearrange("(g p j) w -> p g j w", p=P, j=J)
    o0_v = out_0.rearrange("(g p j) w -> p g j w", p=P, j=J)
    k_v = kernel.rearrange("(a p) c -> p a c", p=P)
    o1_v = out_1.rearrange("(a p) c -> p a c", p=P)

    with ExitStack() as ctx:
        keep = ctx.enter_context(tc.tile_pool(name="keep", bufs=1))
        st = ctx.enter_context(tc.tile_pool(name="st", bufs=6))
        ilv = ctx.enter_context(tc.tile_pool(name="ilv", bufs=3))
        gpool = ctx.enter_context(tc.tile_pool(name="gpool", bufs=2))
        ppool = ctx.enter_context(tc.tile_pool(name="ppool", bufs=RING))
        rpool = ctx.enter_context(tc.tile_pool(name="rpool", bufs=RING))
        dzpool = ctx.enter_context(tc.tile_pool(name="dzpool", bufs=2))
        tgpool = ctx.enter_context(tc.tile_pool(name="tgpool", bufs=2))
        tcpool = ctx.enter_context(tc.tile_pool(name="tcpool", bufs=2))
        psum = ctx.enter_context(tc.psum_pool(name="psum", bufs=1))
        ctx.enter_context(tc.manual_schedule())

        def bank(b, shape, dtype, nm):
            return psum.tile(shape, dtype, name="%s_b%d" % (nm, b), tag="b%d" % b)


        one = keep.tile([P, 1], F32, name="one")
        nc.vector.memset(one[:], 1.0)
        warm = keep.tile([P, 1], F32, name="warm")
        nc.scalar.activation(out=warm[:], in_=one[:], func=ACT.Sqrt)
        ident_b = keep.tile([P, P], BF16, name="ident_b")
        make_identity(nc, ident_b[:])
        ident_f = keep.tile([P, P], F32, name="ident_f")
        make_identity(nc, ident_f[:])

        junk_v = keep.tile([P, C], F32, name="junk_v")
        junk_s = keep.tile([P, C], BF16, name="junk_s")

        ktn = keep.tile([P, NB, D], BF16, name="ktn")
        ktc = keep.tile([P, NH, D], U32, name="ktc", align_bytes=64)
        kts = keep.tile([P, NH, D], U8, name="kts", align_bytes=64)
        xc = keep.tile([P, NG, D], U32, name="xc", align_bytes=64)
        xs = keep.tile([P, NG, D], U8, name="xs", align_bytes=64)
        dzc = keep.tile([P, NG, C], U32, name="dzc", align_bytes=64)
        dzs = keep.tile([P, NG, C], U8, name="dzs", align_bytes=64)
        rkb = keep.tile([P, C], F32, name="rkb")

        ssk = keep.tile([P, 16], F32, name="ssk")
        tk = keep.tile([P, 16], F32, name="tk")
        nrk2 = keep.tile([P, 16], F32, name="nrk2")
        rk2 = keep.tile([P, 16], F32, name="rk2")
        rx2 = keep.tile([P, NT], F32, name="rx2")
        tjunk = keep.tile([P, 8], F32, name="tjunk")
        rk10 = keep.tile([P, 16], F32, name="rk10")
        ssx = keep.tile([P, NT], F32, name="ssx")
        tx = keep.tile([P, NT], F32, name="tx")
        nrx2 = keep.tile([P, NT], F32, name="nrx2")
        rx = keep.tile([P, NT], F32, name="rx")
        s_all = keep.tile([P, NT], F32, name="s_all")
        sg2 = keep.tile([P, 2 * NT], F32, name="sg2")
        sg = keep.tile([P, NT], F32, name="sg")
        cg2 = keep.tile([P, 16], F32, name="cg2")
        cg = keep.tile([P, 8], F32, name="cg")
        sgs = keep.tile([P, 16], F32, name="sgs")

        nc.vector.memset(ssk[:], 1.0)

        def kcol(m):
            return m if m < NGRAM else m + 2

        xr = [keep.tile([P, J, D], BF16, name="xr%d" % g) for g in range(NG)]
        gr = [None] * NG
        pt = [None] * NT
        rb = [None] * NT
        kraw = [None] * NCHUNK

        def load_x(g, j0, j1):
            nc.sync.dma_start(out=xr[g][:, j0:j1, :], in_=x_v[:, g, j0:j1, :])

        def alloc_g(g):
            gr[g] = gpool.tile([P, J, C], BF16, name="gr", tag="gr")

        def load_g(g, j0, j1):
            nc.sync.dma_start(out=gr[g][:, j0:j1, :], in_=go_v[:, g, j0:j1, :])

        def load_p(r):
            pt[r] = ppool.tile([P, C], F32, name="pt", tag="pt")
            nc.sync.dma_start(out=pt[r][:], in_=pr_v[:, r // J, r % J, :])

        def load_r(r):
            rb[r] = rpool.tile([P, C], F32, name="rb", tag="rb")
            nc.sync.dma_start(out=rb[r][:], in_=rb_v[:, r // J, r % J, :])

        def load_tile(r):
            load_r(r)
            load_p(r)

        alloc_g(0)
        alloc_g(1)
        for ch in range(NCHUNK):
            kraw[ch] = st.tile([P, 2, C], BF16, name="kraw%d" % ch, tag="st")
            nc.sync.dma_start(out=kraw[ch][:], in_=k_v[:, 2 * ch : 2 * ch + 2, :])
        load_x(0, 0, 2)
        load_tile(0)
        load_g(0, 0, 2)
        load_tile(1)
        load_tile(2)
        load_x(0, 2, 4)
        load_g(0, 2, 4)
        load_tile(3)
        load_x(1, 0, 4)
        load_tile(4)
        load_g(1, 0, 4)
        load_tile(5)
        load_x(2, 0, 4)

        def loads_after(r):
            if r + RING < NT:
                load_p(r + RING)
                load_r(r + RING)

        def rx_sq(r):
            nc.scalar.activation(out=junk_s[:], in_=xr[r // J][:, r % J, :], func=ACT.Square, accum_out=ssx[:, r : r + 1])

        def rx_fin(c0, c1):
            nc.vector.tensor_scalar(out=tx[:, c0:c1], in0=ssx[:, c0:c1], scalar1=EPS, scalar2=None, op0=ALU.max, op1=ALU.add, accum_out=tjunk[:, 0:1])
            nc.vector.reciprocal(out=rx2[:, c0:c1], in_=tx[:, c0:c1])
            nc.scalar.activation(out=rx[:, c0:c1], in_=rx2[:, c0:c1], func=ACT.Sqrt)
            nc.scalar.activation(out=nrx2[:, c0:c1], in_=rx2[:, c0:c1], func=ACT.Copy, scale=-1.0)

        gps = [None] * NT
        rp = []
        dz = [None] * NG
        dzg = [None] * NG
        xg = [None] * NG
        tgp = [None] * (NPAIR + 2)
        tcd = [None] * NPAIR
        tsc = [None] * NPAIR
        aps = [None] * NT
        dx = [None] * NT
        tps = {}

        def g_mul1(r):
            nc.gpsimd.tensor_tensor(out=rb[r][:, 0:C], in0=rb[r][:, 0:C], in1=pt[r][:, 0:C], op=ALU.mult)

        def g_mul2(r):
            nc.gpsimd.tensor_tensor(out=rb[r][:, 0:C], in0=rb[r][:, 0:C], in1=rkb[:, 0:C], op=ALU.mult)

        def g_mul(r):
            g_mul1(r)
            g_mul2(r)

        def s_scale(r):
            nc.scalar.activation(out=rb[r][:], in_=rb[r][:], func=ACT.Copy, scale=rx[:, r : r + 1])

        def v_mul(r):
            nc.vector.scalar_tensor_tensor(out=rb[r][:], in0=pt[r][:], scalar=rx[:, r : r + 1], in1=rb[r][:], op0=ALU.mult, op1=ALU.mult)

        def gcopy(r):
            gps[r] = bank(r % 2, [P, C], BF16, "gps")
            for n in range(NH):
                nc.tensor.matmul(out=gps[r][:, H * n : H * n + H], lhsT=ident_b[:], rhs=gr[r // J][:, r % J, H * n : H * n + H], start=True, stop=True)

        def row_sum(r):
            nc.vector.scalar_tensor_tensor(out=junk_v[:], in0=gps[r][:], scalar=1.0, in1=pt[r][:], op0=ALU.mult, op1=ALU.mult, accum_out=s_all[:, r : r + 1])

        def alloc_dz(r):
            if r % J == 0:
                dz[r // J] = dzpool.tile([P, J, C], BF16, name="dz", tag="dz")

        def make_dz(r):
            alloc_dz(r)
            nc.vector.scalar_tensor_tensor(out=dz[r // J][:, r % J, :], in0=gps[r][:], scalar=s_all[:, r : r + 1], in1=rb[r][:], op0=ALU.subtract, op1=ALU.mult)

        def make_dz_without_rk(r):
            nc.vector.scalar_tensor_tensor(out=rb[r][:], in0=gps[r][:], scalar=s_all[:, r : r + 1], in1=rb[r][:], op0=ALU.subtract, op1=ALU.mult)

        def times_rk(r):
            alloc_dz(r)
            for n in range(NH):
                nc.vector.tensor_tensor(out=dz[r // J][:, r % J, H * n : H * n + H], in0=rb[r][:, H * n : H * n + H], in1=rp[n][:], op=ALU.mult)

        def alloc_tgp(d):
            tgp[d] = tgpool.tile([P, 2, NH, P, J], BF16, name="tgp", tag="tgp", align_bytes=64)

        def transpose_dz(r):
            tps[r] = bank(2 + r % 2, [P, NH, 2, P], F32, "tps")
            w = dz[r // J][:, r % J, :].bitcast(F32)
            for h in range(NH):
                for u in range(2):
                    nc.tensor.transpose(tps[r][:, h, u, :], w[:, WORDS * h + u : WORDS * (h + 1) : 2], ident_f[:])

        def copy_dz_t(r):
            dst = tgp[r // 2][:, r % 2].rearrange("q h p t -> q (h p t)").bitcast(F32).rearrange("q (h p u) -> q h p u", h=NH, u=2)
            nc.scalar.copy(out=dst, in_=tps[r][:].rearrange("q h u p -> q h p u"))

        def quantize_pair(d):
            tcd[d] = tcpool.tile([P, 2 * NH * P], U32, name="tcd", tag="tcd", align_bytes=64)
            tsc[d] = tcpool.tile([P, 2 * NH * P], U8, name="tsc", tag="tsc", align_bytes=64)
            nc.vector.quantize_mx(out=tcd[d][:].bitcast(E5), scales=tsc[d][:], in_=tgp[d][:].rearrange("q i h p t -> q (i h p t)"))
            alloc_tgp(d + 2)
            nc.gpsimd.memset(tgp[d + 2][:, 0, 0, 0:4, :], 0.0)

        def product_a(r, b0):
            aps[r] = [bank(b0, [P, H], F32, "aps"), bank(b0 + 1, [P, H], F32, "aps")]
            for n in range(NH):
                for h in range(NH):
                    c0 = P * (NH * (r % 2) + h)
                    nc.tensor.matmul_mx(
                        out=aps[r][n][:],
                        lhsT=tcd[r // 2][:, c0 : c0 + P].bitcast(E5),
                        lhsT_scale=tsc[r // 2][:, c0 : c0 + P],
                        rhs=ktc[:, h, H * n : H * n + H].bitcast(E4),
                        rhs_scale=kts[:, h, H * n : H * n + H],
                        start=(h == 0),
                        stop=(h == NH - 1),
                    )

        def x_row(r):
            return xr[r // J][:, r % J, :]

        def project_sum(r):
            for n in range(NH):
                nc.vector.scalar_tensor_tensor(out=junk_v[:, 0:H], in0=aps[r][n][:], scalar=nrx2[:, r : r + 1], in1=x_row(r)[:, H * n : H * n + H], op0=ALU.mult, op1=ALU.mult, accum_out=sg2[:, 2 * r + n : 2 * r + n + 1])
            nc.scalar.activation(out=sg[:, r : r + 1], in_=sg2[:, 2 * r : 2 * r + 1], func=ACT.Identity, bias=sg2[:, 2 * r + 1 : 2 * r + 2])

        def project(r):
            dx[r] = st.tile([P, D], F32, name="dx", tag="st")
            for n in range(NH):
                nc.vector.scalar_tensor_tensor(out=dx[r][:, H * n : H * n + H], in0=x_row(r)[:, H * n : H * n + H], scalar=sg[:, r : r + 1], in1=aps[r][n][:], op0=ALU.mult, op1=ALU.add)
            nc.sync.dma_start(out=o0_v[:, r // J, r % J, :], in_=dx[r][:])

        asb = {}
        prod = {}

        def far_copy(r):
            asb[r] = ppool.tile([P, D], F32, name="gpa", tag="pt")
            for n in range(NH):
                nc.scalar.copy(out=asb[r][:, H * n : H * n + H], in_=aps[r][n][:])

        def far_product(r):
            prod[r] = rpool.tile([P, D], F32, name="gpp", tag="rb")
            nc.gpsimd.tensor_tensor(out=prod[r][:], in0=asb[r][:], in1=x_row(r), op=ALU.mult)

        def far_sum(r):
            nc.scalar.activation(out=junk_s[:], in_=prod[r][:], func=ACT.Copy, scale=nrx2[:, r : r + 1], accum_out=sgs[:, r : r + 1])

        def far_project(r):
            dx[r] = st.tile([P, D], F32, name="dx", tag="st")
            nc.gpsimd.tensor_scalar(out=prod[r][:], in0=x_row(r), scalar1=sgs[:, r : r + 1], scalar2=0.0, op0=ALU.mult, op1=ALU.add)
            nc.gpsimd.tensor_tensor(out=dx[r][:], in0=prod[r][:], in1=asb[r][:], op=ALU.add)
            nc.sync.dma_start(out=o0_v[:, r // J, r % J, :], in_=dx[r][:])

        def interleave_dz(g, piece, eng):
            if piece == 0:
                dzg[g] = ilv.tile([P, C, J], BF16, name="dzg", tag="ilv", align_bytes=64)
            ws = slice(PIECE * piece, PIECE * piece + PIECE)
            if eng == "G":
                nc.gpsimd.tensor_scalar(out=dzg[g][:, ws, :], in0=dz[g][:, :, ws].rearrange("p j w -> p w j"), scalar1=1.0, scalar2=0.0, op0=ALU.mult, op1=ALU.add)
            else:
                nc.scalar.copy(out=dzg[g][:, ws, :], in_=dz[g][:, :, ws].rearrange("p j w -> p w j"))

        def quantize_dz(g):
            nc.vector.quantize_mx(out=dzc[:, g, :].bitcast(E5), scales=dzs[:, g, :], in_=dzg[g][:].rearrange("p w j -> p (w j)"))

        def interleave_x(g, piece, eng):
            if piece == 0:
                xg[g] = ilv.tile([P, D, J], BF16, name="xg", tag="ilv", align_bytes=64)
            ws = slice(PIECE * piece, PIECE * piece + PIECE)
            if eng == "G":
                nc.gpsimd.tensor_scalar(out=xg[g][:, ws, :], in0=xr[g][:, :, ws].rearrange("p j w -> p w j"), scalar1=1.0, scalar2=0.0, op0=ALU.mult, op1=ALU.add)
            else:
                nc.scalar.copy(out=xg[g][:, ws, :], in_=xr[g][:, :, ws].rearrange("p j w -> p w j"))

        def quantize_x(g):
            nc.vector.quantize_mx(out=xc[:, g, :].bitcast(E4), scales=xs[:, g, :], in_=xg[g][:].rearrange("p w j -> p (w j)"))

        ring = [6, 7, 4, 5]
        ring_at = [0]
        ktg = [None] * NH
        tb = {}
        kb = {}

        def next_bank():
            b = ring[ring_at[0] % 4]
            ring_at[0] = ring_at[0] + 1
            return b

        def transpose_k_words(h, ch):
            tb[(h, ch)] = bank(next_bank(), [P, 2, 2, P], F32, "tb")
            for a2 in range(2):
                kw = kraw[ch][:, a2, :].bitcast(F32)
                for u in range(2):
                    nc.tensor.transpose(tb[(h, ch)][:, a2, u, :], kw[:, WORDS * h + u : WORDS * (h + 1) : 2], ident_f[:])

        def copy_k_words(h, ch, eng):
            if ch == 0:
                ktg[h] = ilv.tile([P, D, J], BF16, name="ktg", tag="ilv", align_bytes=64)
            ktw = ktg[h][:].rearrange("q f t -> q (f t)").bitcast(F32)
            dst = ktw[:, H * ch : H * ch + H].rearrange("q (a f u) -> q a f u", a=2, u=2)
            if eng == "V":
                nc.vector.tensor_copy(out=dst, in_=tb[(h, ch)][:].rearrange("q a u f -> q a f u"))
            else:
                nc.scalar.copy(out=dst, in_=tb[(h, ch)][:].rearrange("q a u f -> q a f u"))

        def quantize_k(h):
            nc.vector.quantize_mx(out=ktc[:, h, :].bitcast(E4), scales=kts[:, h, :], in_=ktg[h][:].rearrange("q f t -> q (f t)"))

        def transpose_k_block(m):
            kb[m] = bank(next_bank(), [P, D], BF16, "kb")
            for a in range(NB):
                nc.tensor.transpose(kb[m][:, a * P : (a + 1) * P], kraw[a // 2][:, a % 2, m * P : (m + 1) * P], ident_b[:])

        def copy_k_block(m):
            nc.scalar.copy(out=ktn[:, m, :], in_=kb[m][:])

        cps = [None] * NB
        dk = [None] * NB
        o1 = {}

        def alloc_c(m, b):
            cps[m] = [bank(b[0], [P, H], F32, "cps"), bank(b[1], [P, H], F32, "cps")]

        def product_c(m, gs):
            for n in range(NH):
                for g in gs:
                    nc.tensor.matmul_mx(
                        out=cps[m][n][:],
                        lhsT=dzc[:, g, P * m : P * m + P].bitcast(E5),
                        lhsT_scale=dzs[:, g, P * m : P * m + P],
                        rhs=xc[:, g, H * n : H * n + H].bitcast(E4),
                        rhs_scale=xs[:, g, H * n : H * n + H],
                        start=(g == 0),
                        stop=(g == NG - 1),
                    )

        def c_sum(m, n):
            nc.vector.scalar_tensor_tensor(out=junk_v[:, 0:H], in0=cps[m][n][:], scalar=nrk2[:, kcol(m) : kcol(m) + 1], in1=ktn[:, m, H * n : H * n + H], op0=ALU.mult, op1=ALU.mult, accum_out=cg2[:, 2 * m + n : 2 * m + n + 1])

        def c_total(m):
            nc.vector.tensor_tensor(out=cg[:, m : m + 1], in0=cg2[:, 2 * m : 2 * m + 1], in1=cg2[:, 2 * m + 1 : 2 * m + 2], op=ALU.add)

        def c_project(m, n):
            if n == 0:
                dk[m] = st.tile([P, D], F32, name="dk", tag="st")
            nc.vector.scalar_tensor_tensor(out=dk[m][:, H * n : H * n + H], in0=ktn[:, m, H * n : H * n + H], scalar=cg[:, m : m + 1], in1=cps[m][n][:], op0=ALU.mult, op1=ALU.add)

        def c_store(m):
            o1[m] = rpool.tile([P, NB, P], F32, name="o1s", tag="rb")
            b0 = 6 if m < 6 else (4 if m == 6 else 0)
            for hf in range(2):
                bt = bank(b0 + hf, [P, 4, P], F32, "bt")
                for a in range(4):
                    nc.tensor.transpose(bt[:, a, :], dk[m][:, P * (4 * hf + a) : P * (4 * hf + a) + P], ident_f[:])
                if m == NB - 1:
                    nc.vector.tensor_copy(out=o1[m][:, 4 * hf : 4 * hf + 4, :], in_=bt[:])
                    nc.sync.dma_start(out=o1_v[:, 4 * hf : 4 * hf + 4, P * m : P * m + P], in_=o1[m][:, 4 * hf : 4 * hf + 4, :])
                else:
                    nc.scalar.copy(out=o1[m][:, 4 * hf : 4 * hf + 4, :], in_=bt[:])
            if m < NB - 1:
                nc.scalar.dma_start(out=o1_v[:, :, P * m : P * m + P], in_=o1[m][:])

        gb = [bank(m, [P, P], F32, "gb") for m in range(NGRAM)]
        for m in range(NGRAM, NB):
            kb[m] = bank(m, [P, D], BF16, "kb")
        for a in range(NB):
            ka = kraw[a // 2][:, a % 2, :]
            for m in range(NGRAM):
                nc.tensor.matmul(out=gb[m][:], lhsT=ka[:, m * P : (m + 1) * P], rhs=ka[:, m * P : (m + 1) * P], start=(a == 0), stop=(a == NB - 1))
            for m in range(NGRAM, NB):
                nc.tensor.transpose(kb[m][:, a * P : (a + 1) * P], ka[:, m * P : (m + 1) * P], ident_b[:])
        rx_sq(0)
        rx_sq(1)
        nc.scalar.activation(out=junk_s[:], in_=kb[6][:], func=ACT.Square, accum_out=ssk[:, kcol(6) : kcol(6) + 1])
        for m in range(NGRAM):
            nc.vector.scalar_tensor_tensor(out=junk_v[:, 0:P], in0=gb[m][:], scalar=1.0, in1=ident_f[:], op0=ALU.mult, op1=ALU.mult, accum_out=ssk[:, m : m + 1])
        rx_fin(0, 2)
        nc.scalar.activation(out=junk_s[:], in_=kb[7][:], func=ACT.Square, accum_out=ssk[:, kcol(7) : kcol(7) + 1])
        gcopy(0)
        gcopy(1)
        v_mul(0)
        for m in range(NGRAM, NB):
            copy_k_block(m)
        row_sum(0)
        nc.vector.tensor_scalar(out=tk[:], in0=ssk[:], scalar1=EPS, scalar2=None, op0=ALU.max, op1=ALU.add, accum_out=tjunk[:, 1:2])
        nc.vector.reciprocal(out=rk2[:], in_=tk[:])
        nc.scalar.activation(out=rk10[:], in_=rk2[:], func=ACT.Sqrt, scale=100.0)
        nc.scalar.activation(out=nrk2[:], in_=rk2[:], func=ACT.Copy, scale=-1.0)
        transpose_k_words(0, 0)
        transpose_k_words(0, 1)
        rp.append(bank(4, [P, H], F32, "rp"))
        rp.append(bank(5, [P, H], F32, "rp"))
        for m in range(NB):
            nc.tensor.transpose(rp[m // 4][:, (m % 4) * P : (m % 4 + 1) * P], rk10[:, kcol(m) : kcol(m) + 1].to_broadcast([P, P]), ident_f[:])
        v_mul(1)
        make_dz_without_rk(0)
        nc.scalar.copy(out=rkb[:, 0:H], in_=rp[0][:])
        nc.scalar.copy(out=rkb[:, H:C], in_=rp[1][:])
        row_sum(1)
        g_mul(2)
        alloc_tgp(0)
        alloc_tgp(1)
        gcopy(2)
        times_rk(0)
        loads_after(0)
        transpose_dz(0)
        rx_sq(2)
        rx_sq(3)
        make_dz_without_rk(1)
        gcopy(3)
        times_rk(1)
        loads_after(1)
        transpose_dz(1)
        copy_dz_t(0)
        rx_fin(2, 4)
        g_mul(3)
        s_scale(2)
        transpose_k_words(0, 2)
        transpose_k_words(0, 3)
        row_sum(2)
        row_sum(3)
        rx_sq(4)
        copy_dz_t(1)
        rx_sq(5)
        rx_sq(6)
        make_dz(2)
        loads_after(2)
        transpose_dz(2)
        g_mul(4)
        for ch in range(NCHUNK):
            copy_k_words(0, ch, "V")
            transpose_k_words(1, ch)
        s_scale(3)
        copy_dz_t(2)
        rx_sq(7)
        quantize_k(0)
        make_dz(3)
        loads_after(3)
        alloc_g(2)
        load_g(2, 0, 4)
        gcopy(4)
        transpose_dz(3)
        gcopy(5)
        for ch in range(3):
            copy_k_words(1, ch, "S")
            transpose_k_block(ch)
        copy_dz_t(3)
        copy_k_words(1, 3, "S")
        transpose_k_block(3)
        quantize_pair(0)
        g_mul(5)
        rx_fin(4, 8)
        row_sum(4)
        row_sum(5)
        for m in range(4):
            copy_k_block(m)
            if m + 4 < NGRAM:
                transpose_k_block(m + 4)
        for m in range(4, NGRAM):
            copy_k_block(m)
        quantize_k(1)
        quantize_pair(1)
        product_a(0, 4)
        product_a(1, 6)
        g_mul(6)
        g_mul(7)

        for d in range(2, NPAIR):
            lo, hi = 2 * d, 2 * d + 1
            project_sum(lo - 4)
            project_sum(hi - 4)
            if d == 4:
                rx_fin(8, 12)
            if d % 2 == 1:
                quantize_dz(d // 2 - 1)
            if d > 2:
                quantize_pair(d - 1)
            project(lo - 4)
            project(hi - 4)
            product_a(lo - 2, 4)
            product_a(hi - 2, 6)
            if hi + 4 < NT:
                g_mul(lo + 4)
                g_mul(hi + 4)
            else:
                for piece in range(4):
                    interleave_x(d - 4, piece, "G")
            if d % 2 == 0:
                interleave_dz(d // 2 - 1, 0, "S")
            s_scale(lo)
            s_scale(hi)
            if d % 2 == 0:
                for piece in range(1, 4):
                    interleave_dz(d // 2 - 1, piece, "S")
            if d == 3:
                for r in range(8, 12):
                    rx_sq(r)
            if d == 5:
                for piece in range(4):
                    interleave_x(2, piece, "S")
            if d > 2:
                row_sum(lo)
                row_sum(hi)
            for r in (lo, hi):
                make_dz(r)
                loads_after(r)
                transpose_dz(r)
                copy_dz_t(r)
            if d + 1 < NPAIR:
                gcopy(lo + 2)
                gcopy(hi + 2)

        pairs_of_banks = [(0, 1), (2, 3), (4, 5)]
        interleave_dz(2, 0, "S")
        interleave_dz(2, 2, "G")
        interleave_dz(2, 1, "S")
        interleave_dz(2, 3, "G")
        project_sum(8)
        project_sum(9)
        quantize_x(0)
        quantize_pair(5)
        project(8)
        project(9)
        product_a(10, 4)
        product_a(11, 6)
        quantize_x(1)
        far_copy(10)
        far_copy(11)
        far_product(10)
        far_product(11)
        for m in range(3):
            alloc_c(m, pairs_of_banks[m])
            product_c(m, (0, 1))
        quantize_dz(2)
        quantize_x(2)
        far_sum(10)
        far_sum(11)
        for m in range(3):
            product_c(m, (2,))
        far_project(10)
        far_project(11)
        c_sum(0, 0)
        c_sum(0, 1)
        for m in range(NB):
            if m + 1 < NB:
                c_sum(m + 1, 0)
            c_total(m)
            if m + 1 < NB:
                c_sum(m + 1, 1)
            c_project(m, 0)
            c_project(m, 1)
            if m + 3 < NB:
                alloc_c(m + 3, pairs_of_banks[m % 3])
                product_c(m + 3, (0, 1, 2))
            c_store(m)
